import numpy as np
import ml_dtypes

BF16 = ml_dtypes.bfloat16


def bf(x):
    return np.asarray(x, np.float32).astype(BF16)


def f32(x):
    return np.asarray(x, np.float32)


def f64(x):
    return np.asarray(x).astype(np.float64)


def striped(idx):
    return np.tile(idx.reshape(-1, 16).T, (8, 1))


D, S, NODES, NEI, N, H, RUNS = 128, 1024, 128, 16, 2048, 512, 4
SLOPE = 0.01


def setup_inputs():
    idx = np.concatenate([np.random.permutation(S)[:H] for _ in range(RUNS)])
    return {"table": bf(np.random.standard_normal((D, S))), "h_ref": bf(np.random.standard_normal((D, NODES))), "a_nei": bf(0.1 * np.random.standard_normal((D, 1))), "a_ref": bf(0.1 * np.random.standard_normal((D, 1))), "offs": striped(idx)}


def reference(table, h_ref, a_nei, a_ref, offs):
    idx = offs[:16].T.reshape(-1)
    nei = f64(table)[:, idx]
    score = (f64(a_nei).T @ nei).reshape(NODES, NEI) + (f64(a_ref).T @ f64(h_ref)).reshape(NODES, 1)
    act = np.maximum(score, SLOPE * score)
    e = np.exp(act - act.max(axis=1, keepdims=True))
    att = e / e.sum(axis=1, keepdims=True)
    v = (nei.reshape(D, NODES, NEI) * att[None, :, :]).sum(axis=2)
    return np.maximum(v, 0.0) + np.exp(np.minimum(v, 0.0)) - 1.0

@@ -1,0 +1,99 @@
+import concourse.mybir as mybir
+from concourse.masks import make_identity
+
+BF16 = mybir.dt.bfloat16
+F32 = mybir.dt.float32
+U16 = mybir.dt.uint16
+ALU = mybir.AluOpType
+ACT = mybir.ActivationFunctionType
+X = mybir.AxisListType.X
+
+D = 128
+S = 1024
+NODES = 128
+NEI = 16
+N = NODES * NEI
+PIECE = 512
+PIECES = N // PIECE
+PIECE_NODES = PIECE // NEI
+PIECE_COLS = PIECE // 16
+SLOPE = 0.01
+
+FLOPS = 2 * D * N + 2 * D * NODES + 2 * D * N
+
+
+def tile_sc_encoder_kernel(tc, table, h_ref, a_nei, a_ref, offs, out):
+    nc = tc.nc
+    with (
+        tc.tile_pool(name="held", bufs=1) as held,
+        tc.tile_pool(name="work", bufs=2) as work,
+        tc.psum_pool(name="psum", bufs=1) as psum,
+    ):
+        offsets = held.tile([128, N // 16], U16, name="offsets")
+        nc.sync.dma_start(offsets[:], offs)
+        table_sb = held.tile([D, S], BF16, name="table_sb")
+        nc.scalar.dma_start(table_sb[:], table)
+        href_sb = held.tile([D, NODES], BF16, name="href_sb")
+        nc.sync.dma_start(href_sb[:], h_ref)
+        anei_sb = held.tile([D, 1], BF16, name="anei_sb")
+        nc.sync.dma_start(anei_sb[:], a_nei)
+        aref_sb = held.tile([D, 1], BF16, name="aref_sb")
+        nc.sync.dma_start(aref_sb[:], a_ref)
+
+        w_nei = held.tile([D, 128], BF16, name="w_nei")
+        nc.vector.tensor_copy(w_nei[:], anei_sb[:, 0:1].to_broadcast([D, 128]))
+        w_ref = held.tile([D, 128], BF16, name="w_ref")
+        nc.vector.tensor_copy(w_ref[:], aref_sb[:, 0:1].to_broadcast([D, 128]))
+        ident = held.tile([D, D], BF16, name="ident")
+        make_identity(nc, ident[:])
+
+        esum = held.tile([D, NODES], F32, name="esum")
+        rsum = held.tile([D, NODES], F32, name="rsum")
+        vsum = held.tile([D, NODES], F32, name="vsum")
+
+        scores = [psum.tile([D, PIECE_NODES, NEI], F32, name=f"score{r}") for r in range(PIECES)]
+        feats = [psum.tile([D, PIECE_NODES, NEI], F32, name=f"feat{r}") for r in range(PIECES)]
+        for r in range(PIECES):
+            nodes = slice(r * PIECE_NODES, (r + 1) * PIECE_NODES)
+            href_rep = href_sb[:, nodes].unsqueeze(2).to_broadcast([D, PIECE_NODES, NEI])
+            nc.tensor.matmul(scores[r][:], w_ref[:], href_rep, start=True, stop=False)
+        for r in range(PIECES):
+            looked_up = table_sb[:].indirect(offsets[:, r * PIECE_COLS : (r + 1) * PIECE_COLS])
+            nc.tensor.matmul(scores[r][:].rearrange("p n t -> p (n t)"), w_nei[:], looked_up, start=False, stop=True)
+            nc.tensor.matmul(feats[r][:].rearrange("p n t -> p (n t)"), ident[:], looked_up, start=True, stop=True)
+
+        for r in range(PIECES):
+            nodes = slice(r * PIECE_NODES, (r + 1) * PIECE_NODES)
+            score = scores[r]
+            feat = feats[r]
+
+            damped = work.tile([D, PIECE_NODES, NEI], F32, name="damped")
+            nc.scalar.mul(damped[:], score[:], SLOPE)
+            act = work.tile([D, PIECE_NODES, NEI], F32, name="act")
+            nc.vector.tensor_tensor(act[:], score[:], damped[:], op=ALU.max)
+
+            top = work.tile([D, PIECE_NODES], F32, name="top")
+            nc.vector.tensor_reduce(top[:], act[:], axis=X, op=ALU.max)
+            shifted = work.tile([D, PIECE_NODES, NEI], F32, name="shifted")
+            top_rep = top[:].unsqueeze(2).to_broadcast([D, PIECE_NODES, NEI])
+            nc.vector.tensor_tensor(shifted[:], act[:], top_rep, op=ALU.subtract)
+            e = work.tile([D, PIECE_NODES, NEI], F32, name="e")
+            nc.scalar.activation(e[:], shifted[:], ACT.Exp)
+            nc.vector.tensor_reduce(esum[:, nodes], e[:], axis=X, op=ALU.add)
+            nc.vector.reciprocal(rsum[:, nodes], esum[:, nodes])
+
+            prod = work.tile([D, PIECE_NODES, NEI], F32, name="prod")
+            nc.vector.tensor_tensor(prod[:], feat[:], e[:], op=ALU.mult)
+            nc.vector.tensor_reduce(vsum[:, nodes], prod[:], axis=X, op=ALU.add)
+
+        v = held.tile([D, NODES], F32, name="v")
+        nc.vector.tensor_tensor(v[:], vsum[:], rsum[:], op=ALU.mult)
+        neg = held.tile([D, NODES], F32, name="neg")
+        nc.vector.tensor_scalar_min(neg[:], v[:], 0.0)
+        eneg = held.tile([D, NODES], F32, name="eneg")
+        nc.scalar.activation(eneg[:], neg[:], ACT.Exp)
+        pos = held.tile([D, NODES], F32, name="pos")
+        nc.vector.tensor_scalar(pos[:], v[:], 0.0, -1.0, op0=ALU.max, op1=ALU.add)
+        res = held.tile([D, NODES], F32, name="res")
+        nc.vector.tensor_tensor(res[:], pos[:], eneg[:], op=ALU.add)
+        nc.sync.dma_start(out, res[:])

@@ -13,11 +13,20 @@ S = 1024
 NODES = 128
 NEI = 16
 N = NODES * NEI
+SLOPE = 0.01
+
+GROUPS = 8
+G_PARTS = 128 // GROUPS
+G_NODES = NODES // GROUPS
+G_COLS = G_NODES * NEI // 16
+
+WARM_UP = 4
+
 PIECE = 512
 PIECES = N // PIECE
-PIECE_NODES = PIECE // NEI
-PIECE_COLS = PIECE // 16
-SLOPE = 0.01
+P_NODES = PIECE // NEI
+P_COLS = PIECE // 16
+P_GROUPS = GROUPS // PIECES
 
 FLOPS = 2 * D * N + 2 * D * NODES + 2 * D * N
 
@@ -28,72 +37,106 @@ def tile_sc_encoder_kernel(tc, table, h_ref, a_nei, a_ref, offs, out):
         tc.tile_pool(name="held", bufs=1) as held,
         tc.tile_pool(name="work", bufs=2) as work,
         tc.psum_pool(name="psum", bufs=1) as psum,
+        tc.psum_pool(name="psum_rot", bufs=2) as psum_rot,
     ):
-        offsets = held.tile([128, N // 16], U16, name="offsets")
-        nc.sync.dma_start(offsets[:], offs)
-        table_sb = held.tile([D, S], BF16, name="table_sb")
-        nc.scalar.dma_start(table_sb[:], table)
-        href_sb = held.tile([D, NODES], BF16, name="href_sb")
-        nc.sync.dma_start(href_sb[:], h_ref)
-        anei_sb = held.tile([D, 1], BF16, name="anei_sb")
-        nc.sync.dma_start(anei_sb[:], a_nei)
+        zeros = held.tile([128, PIECE], BF16, name="zeros")
+        nc.vector.memset(zeros[:], 0.0)
+
         aref_sb = held.tile([D, 1], BF16, name="aref_sb")
         nc.sync.dma_start(aref_sb[:], a_ref)
+        href_sb = held.tile([D, NODES], BF16, name="href_sb")
+        nc.scalar.dma_start(href_sb[:], h_ref)
+        table_sb = held.tile([D, S], BF16, name="table_sb")
+        nc.scalar.dma_start(table_sb[:, 0 : S // 2], table[:, 0 : S // 2])
+        anei_sb = held.tile([D, 1], BF16, name="anei_sb")
+        nc.sync.dma_start(anei_sb[:], a_nei)
+        offsets = held.tile([128, N // 16], U16, name="offsets")
+        nc.sync.dma_start(offsets[:], offs)
+        nc.sync.dma_start(table_sb[:, S // 2 : S], table[:, S // 2 : S])
 
-        w_nei = held.tile([D, 128], BF16, name="w_nei")
-        nc.vector.tensor_copy(w_nei[:], anei_sb[:, 0:1].to_broadcast([D, 128]))
-        w_ref = held.tile([D, 128], BF16, name="w_ref")
-        nc.vector.tensor_copy(w_ref[:], aref_sb[:, 0:1].to_broadcast([D, 128]))
+        in_group = held.tile([D, GROUPS, 128], BF16, name="in_group")
+        nc.vector.memset(in_group[:], 0.0)
+        for g in range(GROUPS):
+            nc.vector.memset(in_group[:, g, g * G_PARTS : (g + 1) * G_PARTS], 1.0)
         ident = held.tile([D, D], BF16, name="ident")
         make_identity(nc, ident[:])
+        pick = held.tile([128, GROUPS, D], F32, name="pick")
+        first_of_group = ident[:].rearrange("k (g i) -> k g i", i=G_PARTS)[:, :, 0:1]
+        nc.gpsimd.tensor_copy(pick[:], first_of_group.to_broadcast([128, GROUPS, D]))
+        ones = held.tile([128, D], F32, name="ones")
+        nc.gpsimd.memset(ones[:], 1.0)
 
-        esum = held.tile([D, NODES], F32, name="esum")
-        rsum = held.tile([D, NODES], F32, name="rsum")
-        vsum = held.tile([D, NODES], F32, name="vsum")
+        w_ref = held.tile([D, GROUPS, 128], BF16, name="w_ref")
+        nc.vector.tensor_scalar_mul(w_ref[:], in_group[:], aref_sb[:, 0:1])
+        w_nei = held.tile([D, GROUPS, 128], BF16, name="w_nei")
+        nc.vector.tensor_scalar_mul(w_nei[:], in_group[:], anei_sb[:, 0:1])
 
-        scores = [psum.tile([D, PIECE_NODES, NEI], F32, name=f"score{r}") for r in range(PIECES)]
-        feats = [psum.tile([D, PIECE_NODES, NEI], F32, name=f"feat{r}") for r in range(PIECES)]
+        feats = [psum.tile([D, P_NODES, NEI], F32, name=f"feat{r}") for r in range(PIECES)]
+        for i in range(WARM_UP):
+            nc.tensor.matmul(
+                feats[i % PIECES][:].rearrange("p n t -> p (n t)"), zeros[:, 0:128], zeros[:], start=True, stop=True
+            )
+
+        score = psum.tile([128, G_NODES, NEI], F32, name="score")
+        for g in range(GROUPS):
+            href_rep = href_sb[:, g * G_NODES : (g + 1) * G_NODES].unsqueeze(2).to_broadcast([D, G_NODES, NEI])
+            nc.tensor.matmul(score[:], w_ref[:, g, :], href_rep, start=(g == 0), stop=False)
+        for g in range(GROUPS):
+            looked_up = table_sb[:].indirect(offsets[:, g * G_COLS : (g + 1) * G_COLS])
+            nc.tensor.matmul(
+                score[:].rearrange("p n t -> p (n t)"), w_nei[:, g, :], looked_up, start=False, stop=(g == GROUPS - 1)
+            )
         for r in range(PIECES):
-            nodes = slice(r * PIECE_NODES, (r + 1) * PIECE_NODES)
-            href_rep = href_sb[:, nodes].unsqueeze(2).to_broadcast([D, PIECE_NODES, NEI])
-            nc.tensor.matmul(scores[r][:], w_ref[:], href_rep, start=True, stop=False)
-        for r in range(PIECES):
-            looked_up = table_sb[:].indirect(offsets[:, r * PIECE_COLS : (r + 1) * PIECE_COLS])
-            nc.tensor.matmul(scores[r][:].rearrange("p n t -> p (n t)"), w_nei[:], looked_up, start=False, stop=True)
+            looked_up = table_sb[:].indirect(offsets[:, r * P_COLS : (r + 1) * P_COLS])
             nc.tensor.matmul(feats[r][:].rearrange("p n t -> p (n t)"), ident[:], looked_up, start=True, stop=True)
 
+        damped = held.tile([128, G_NODES, NEI], F32, name="damped")
+        nc.scalar.mul(damped[:], score[:], SLOPE)
+        top_score = held.tile([128, G_NODES], F32, name="top_score")
+        nc.vector.tensor_reduce(top_score[:], score[:], axis=X, op=ALU.max)
+        act = held.tile([128, G_NODES, NEI], F32, name="act")
+        nc.vector.tensor_tensor(act[:], score[:], damped[:], op=ALU.max)
+        top = held.tile([128, G_NODES], F32, name="top")
+        nc.vector.scalar_tensor_tensor(top[:], top_score[:], SLOPE, top_score[:], op0=ALU.mult, op1=ALU.max)
+        shifted = held.tile([128, G_NODES, NEI], F32, name="shifted")
+        nc.vector.tensor_tensor(
+            shifted[:], act[:], top[:].unsqueeze(2).to_broadcast([128, G_NODES, NEI]), op=ALU.subtract
+        )
+        e = held.tile([128, G_NODES, NEI], F32, name="e")
+        nc.scalar.activation(e[:], shifted[:], ACT.Exp)
+        esum = held.tile([128, G_NODES], F32, name="esum")
+        nc.vector.tensor_reduce(esum[:], e[:], axis=X, op=ALU.add)
+        rsum = held.tile([128, G_NODES], F32, name="rsum")
+        nc.vector.reciprocal(rsum[:], esum[:])
+
+        vsum = held.tile([D, NODES], F32, name="vsum")
         for r in range(PIECES):
-            nodes = slice(r * PIECE_NODES, (r + 1) * PIECE_NODES)
-            score = scores[r]
-            feat = feats[r]
-
-            damped = work.tile([D, PIECE_NODES, NEI], F32, name="damped")
-            nc.scalar.mul(damped[:], score[:], SLOPE)
-            act = work.tile([D, PIECE_NODES, NEI], F32, name="act")
-            nc.vector.tensor_tensor(act[:], score[:], damped[:], op=ALU.max)
-
-            top = work.tile([D, PIECE_NODES], F32, name="top")
-            nc.vector.tensor_reduce(top[:], act[:], axis=X, op=ALU.max)
-            shifted = work.tile([D, PIECE_NODES, NEI], F32, name="shifted")
-            top_rep = top[:].unsqueeze(2).to_broadcast([D, PIECE_NODES, NEI])
-            nc.vector.tensor_tensor(shifted[:], act[:], top_rep, op=ALU.subtract)
-            e = work.tile([D, PIECE_NODES, NEI], F32, name="e")
-            nc.scalar.activation(e[:], shifted[:], ACT.Exp)
-            nc.vector.tensor_reduce(esum[:, nodes], e[:], axis=X, op=ALU.add)
-            nc.vector.reciprocal(rsum[:, nodes], esum[:, nodes])
-
-            prod = work.tile([D, PIECE_NODES, NEI], F32, name="prod")
-            nc.vector.tensor_tensor(prod[:], feat[:], e[:], op=ALU.mult)
-            nc.vector.tensor_reduce(vsum[:, nodes], prod[:], axis=X, op=ALU.add)
+            feat_sb = work.tile([D, P_NODES, NEI], F32, name="feat_sb")
+            nc.scalar.copy(feat_sb[:], feats[r][:])
+            e_all = psum_rot.tile([D, P_NODES, NEI], F32, name="e_all")
+            for h in range(P_GROUPS):
+                nc.tensor.matmul(
+                    e_all[:, h * G_NODES : (h + 1) * G_NODES, :], pick[:, r * P_GROUPS + h, :], e[:], start=True, stop=True
+                )
+            prod = work.tile([D, P_NODES, NEI], F32, name="prod")
+            nc.vector.tensor_tensor(prod[:], e_all[:], feat_sb[:], op=ALU.mult)
+            nc.vector.tensor_reduce(vsum[:, r * P_NODES : (r + 1) * P_NODES], prod[:], axis=X, op=ALU.add)
+        rsum_own = held.tile([128, GROUPS, G_NODES], F32, name="rsum_own")
+        nc.vector.tensor_tensor(
+            rsum_own[:],
+            rsum[:].unsqueeze(1).to_broadcast([128, GROUPS, G_NODES]),
+            first_of_group.to_broadcast([128, GROUPS, G_NODES]),
+            op=ALU.mult,
+        )
+        rsum_all = psum.tile([D, NODES], F32, name="rsum_all")
+        nc.tensor.matmul(rsum_all[:], ones[:], rsum_own[:].rearrange("k g n -> k (g n)"), start=True, stop=True)
 
         v = held.tile([D, NODES], F32, name="v")
-        nc.vector.tensor_tensor(v[:], vsum[:], rsum[:], op=ALU.mult)
-        neg = held.tile([D, NODES], F32, name="neg")
-        nc.vector.tensor_scalar_min(neg[:], v[:], 0.0)
-        eneg = held.tile([D, NODES], F32, name="eneg")
-        nc.scalar.activation(eneg[:], neg[:], ACT.Exp)
+        nc.vector.tensor_tensor(v[:], rsum_all[:], vsum[:], op=ALU.mult)
+        exp_v = held.tile([D, NODES], F32, name="exp_v")
+        nc.scalar.activation(exp_v[:], v[:], ACT.Exp)
         pos = held.tile([D, NODES], F32, name="pos")
         nc.vector.tensor_scalar(pos[:], v[:], 0.0, -1.0, op0=ALU.max, op1=ALU.add)
         res = held.tile([D, NODES], F32, name="res")
-        nc.vector.tensor_tensor(res[:], pos[:], eneg[:], op=ALU.add)
+        nc.vector.scalar_tensor_tensor(res[:], exp_v[:], 1.0, pos[:], op0=ALU.min, op1=ALU.add)
         nc.sync.dma_start(out, res[:])

@@ -15,18 +15,19 @@ NEI = 16
 N = NODES * NEI
 SLOPE = 0.01
 
-GROUPS = 8
-G_PARTS = 128 // GROUPS
-G_NODES = NODES // GROUPS
+HALVES = 2
+QUADS = 4
+Q_PARTS = 128 // QUADS
+G_NODES = NODES // (HALVES * QUADS)
 G_COLS = G_NODES * NEI // 16
-
-WARM_UP = 4
 
 PIECE = 512
 PIECES = N // PIECE
 P_NODES = PIECE // NEI
 P_COLS = PIECE // 16
-P_GROUPS = GROUPS // PIECES
+P_GROUPS = P_NODES // G_NODES
+
+WARM_UP = 4
 
 FLOPS = 2 * D * N + 2 * D * NODES + 2 * D * N
 
@@ -36,100 +37,127 @@ def tile_sc_encoder_kernel(tc, table, h_ref, a_nei, a_ref, offs, out):
     with (
         tc.tile_pool(name="held", bufs=1) as held,
         tc.tile_pool(name="work", bufs=2) as work,
-        tc.psum_pool(name="psum", bufs=1) as psum,
-        tc.psum_pool(name="psum_rot", bufs=2) as psum_rot,
+        tc.psum_pool(name="psum_score", bufs=HALVES) as psum_score,
+        tc.psum_pool(name="psum_feat", bufs=PIECES) as psum_feat,
+        tc.psum_pool(name="psum_spread", bufs=2) as psum_spread,
     ):
-        zeros = held.tile([128, PIECE], BF16, name="zeros")
-        nc.vector.memset(zeros[:], 0.0)
+        zeros = held.tile([128, 128], BF16, name="zeros")
+        nc.gpsimd.memset(zeros[:], 0.0)
 
         aref_sb = held.tile([D, 1], BF16, name="aref_sb")
         nc.sync.dma_start(aref_sb[:], a_ref)
-        href_sb = held.tile([D, NODES], BF16, name="href_sb")
-        nc.scalar.dma_start(href_sb[:], h_ref)
-        table_sb = held.tile([D, S], BF16, name="table_sb")
-        nc.scalar.dma_start(table_sb[:, 0 : S // 2], table[:, 0 : S // 2])
         anei_sb = held.tile([D, 1], BF16, name="anei_sb")
-        nc.sync.dma_start(anei_sb[:], a_nei)
+        nc.scalar.dma_start(anei_sb[:], a_nei)
+        table_sb = held.tile([D, S], BF16, name="table_sb")
+        nc.scalar.dma_start(table_sb[:], table)
+        href_sb = held.tile([D, NODES], BF16, name="href_sb")
+        nc.sync.dma_start(href_sb[:], h_ref)
         offsets = held.tile([128, N // 16], U16, name="offsets")
         nc.sync.dma_start(offsets[:], offs)
-        nc.sync.dma_start(table_sb[:, S // 2 : S], table[:, S // 2 : S])
 
-        in_group = held.tile([D, GROUPS, 128], BF16, name="in_group")
-        nc.vector.memset(in_group[:], 0.0)
-        for g in range(GROUPS):
-            nc.vector.memset(in_group[:, g, g * G_PARTS : (g + 1) * G_PARTS], 1.0)
+        in_quad = held.tile([D, QUADS, 128], BF16, name="in_quad")
+        nc.vector.memset(in_quad[:], 0.0)
+        for q in range(QUADS):
+            nc.vector.memset(in_quad[:, q, q * Q_PARTS : (q + 1) * Q_PARTS], 1.0)
         ident = held.tile([D, D], BF16, name="ident")
         make_identity(nc, ident[:])
-        pick = held.tile([128, GROUPS, D], F32, name="pick")
-        first_of_group = ident[:].rearrange("k (g i) -> k g i", i=G_PARTS)[:, :, 0:1]
-        nc.gpsimd.tensor_copy(pick[:], first_of_group.to_broadcast([128, GROUPS, D]))
+        first_of_quad = ident[:].rearrange("k (q i) -> k q i", i=Q_PARTS)[:, :, 0:1]
+        pick = held.tile([128, QUADS, D], F32, name="pick")
+        nc.gpsimd.tensor_copy(pick[:], first_of_quad.to_broadcast([128, QUADS, D]))
         ones = held.tile([128, D], F32, name="ones")
         nc.gpsimd.memset(ones[:], 1.0)
 
-        w_ref = held.tile([D, GROUPS, 128], BF16, name="w_ref")
-        nc.vector.tensor_scalar_mul(w_ref[:], in_group[:], aref_sb[:, 0:1])
-        w_nei = held.tile([D, GROUPS, 128], BF16, name="w_nei")
-        nc.vector.tensor_scalar_mul(w_nei[:], in_group[:], anei_sb[:, 0:1])
+        w_ref = held.tile([D, QUADS, 128], BF16, name="w_ref")
+        nc.vector.tensor_scalar_mul(w_ref[:], in_quad[:], aref_sb[:, 0:1])
+        w_nei = held.tile([D, QUADS, 128], BF16, name="w_nei")
+        nc.vector.tensor_scalar_mul(w_nei[:], in_quad[:], anei_sb[:, 0:1])
 
-        feats = [psum.tile([D, P_NODES, NEI], F32, name=f"feat{r}") for r in range(PIECES)]
+        warm = psum_spread.tile([128, PIECE // 128, 128], F32, name="warm", tag="e_all")
         for i in range(WARM_UP):
             nc.tensor.matmul(
-                feats[i % PIECES][:].rearrange("p n t -> p (n t)"), zeros[:, 0:128], zeros[:], start=True, stop=True
+                warm[:], zeros[:], zeros[:].unsqueeze(1).to_broadcast([128, PIECE // 128, 128]), start=True, stop=True
             )
 
-        score = psum.tile([128, G_NODES, NEI], F32, name="score")
-        for g in range(GROUPS):
-            href_rep = href_sb[:, g * G_NODES : (g + 1) * G_NODES].unsqueeze(2).to_broadcast([D, G_NODES, NEI])
-            nc.tensor.matmul(score[:], w_ref[:, g, :], href_rep, start=(g == 0), stop=False)
-        for g in range(GROUPS):
-            looked_up = table_sb[:].indirect(offsets[:, g * G_COLS : (g + 1) * G_COLS])
-            nc.tensor.matmul(
-                score[:].rearrange("p n t -> p (n t)"), w_nei[:, g, :], looked_up, start=False, stop=(g == GROUPS - 1)
-            )
+        s_ref_ps = psum_spread.tile([128, HALVES, G_NODES], F32, name="s_ref_ps", tag="e_all")
+        for half in range(HALVES):
+            for q in range(QUADS):
+                group = half * QUADS + q
+                nc.tensor.matmul(
+                    s_ref_ps[:, half, :],
+                    w_ref[:, q, :],
+                    href_sb[:, group * G_NODES : (group + 1) * G_NODES],
+                    start=(q == 0),
+                    stop=(q == QUADS - 1),
+                )
+        s_ref = held.tile([128, HALVES, G_NODES], F32, name="s_ref")
+        nc.scalar.copy(s_ref[:], s_ref_ps[:])
+        s_nei = [psum_score.tile([128, G_NODES, NEI], F32, name=f"s_nei{half}", tag="score") for half in range(HALVES)]
+        for half in range(HALVES):
+            for q in range(QUADS):
+                group = half * QUADS + q
+                nc.tensor.matmul(
+                    s_nei[half][:].rearrange("p n t -> p (n t)"),
+                    w_nei[:, q, :],
+                    table_sb[:].indirect(offsets[:, group * G_COLS : (group + 1) * G_COLS]),
+                    start=(q == 0),
+                    stop=(q == QUADS - 1),
+                )
+        feats = [psum_feat.tile([D, P_NODES, NEI], F32, name=f"feat{r}", tag="feat") for r in range(PIECES)]
         for r in range(PIECES):
-            looked_up = table_sb[:].indirect(offsets[:, r * P_COLS : (r + 1) * P_COLS])
-            nc.tensor.matmul(feats[r][:].rearrange("p n t -> p (n t)"), ident[:], looked_up, start=True, stop=True)
+            nc.tensor.matmul(
+                feats[r][:].rearrange("p n t -> p (n t)"),
+                ident[:],
+                table_sb[:].indirect(offsets[:, r * P_COLS : (r + 1) * P_COLS]),
+                start=True,
+                stop=True,
+            )
 
-        damped = held.tile([128, G_NODES, NEI], F32, name="damped")
-        nc.scalar.mul(damped[:], score[:], SLOPE)
-        top_score = held.tile([128, G_NODES], F32, name="top_score")
-        nc.vector.tensor_reduce(top_score[:], score[:], axis=X, op=ALU.max)
-        act = held.tile([128, G_NODES, NEI], F32, name="act")
-        nc.vector.tensor_tensor(act[:], score[:], damped[:], op=ALU.max)
-        top = held.tile([128, G_NODES], F32, name="top")
-        nc.vector.scalar_tensor_tensor(top[:], top_score[:], SLOPE, top_score[:], op0=ALU.mult, op1=ALU.max)
-        shifted = held.tile([128, G_NODES, NEI], F32, name="shifted")
-        nc.vector.tensor_tensor(
-            shifted[:], act[:], top[:].unsqueeze(2).to_broadcast([128, G_NODES, NEI]), op=ALU.subtract
-        )
-        e = held.tile([128, G_NODES, NEI], F32, name="e")
-        nc.scalar.activation(e[:], shifted[:], ACT.Exp)
-        esum = held.tile([128, G_NODES], F32, name="esum")
-        nc.vector.tensor_reduce(esum[:], e[:], axis=X, op=ALU.add)
-        rsum = held.tile([128, G_NODES], F32, name="rsum")
-        nc.vector.reciprocal(rsum[:], esum[:])
+        e = held.tile([128, HALVES, G_NODES, NEI], F32, name="e")
+        for half in range(HALVES):
+            score = work.tile([128, G_NODES, NEI], F32, name="score")
+            nc.vector.tensor_tensor(
+                score[:], s_nei[half][:], s_ref[:, half].unsqueeze(2).to_broadcast([128, G_NODES, NEI]), op=ALU.add
+            )
+            top_score = work.tile([128, G_NODES], F32, name="top_score")
+            nc.vector.tensor_reduce(top_score[:], s_nei[half][:], axis=X, op=ALU.max)
+            act = work.tile([128, G_NODES, NEI], F32, name="act")
+            nc.vector.scalar_tensor_tensor(act[:], score[:], SLOPE, score[:], op0=ALU.mult, op1=ALU.max)
+            nc.vector.tensor_tensor(top_score[:], top_score[:], s_ref[:, half], op=ALU.add)
+            top = work.tile([128, G_NODES], F32, name="top")
+            nc.vector.scalar_tensor_tensor(top[:], top_score[:], SLOPE, top_score[:], op0=ALU.mult, op1=ALU.max)
+            shifted = work.tile([128, G_NODES, NEI], F32, name="shifted")
+            nc.vector.tensor_tensor(
+                shifted[:], act[:], top[:].unsqueeze(2).to_broadcast([128, G_NODES, NEI]), op=ALU.subtract
+            )
+            nc.scalar.activation(e[:, half], shifted[:], ACT.Exp)
 
         vsum = held.tile([D, NODES], F32, name="vsum")
         for r in range(PIECES):
-            feat_sb = work.tile([D, P_NODES, NEI], F32, name="feat_sb")
+            feat_sb = held.tile([D, P_NODES, NEI], F32, name=f"feat_sb{r}")
             nc.scalar.copy(feat_sb[:], feats[r][:])
-            e_all = psum_rot.tile([D, P_NODES, NEI], F32, name="e_all")
-            for h in range(P_GROUPS):
+            e_all = psum_spread.tile([D, P_NODES, NEI], F32, name="e_all", tag="e_all")
+            for k in range(P_GROUPS):
+                half, q = divmod(r * P_GROUPS + k, QUADS)
                 nc.tensor.matmul(
-                    e_all[:, h * G_NODES : (h + 1) * G_NODES, :], pick[:, r * P_GROUPS + h, :], e[:], start=True, stop=True
+                    e_all[:, k * G_NODES : (k + 1) * G_NODES, :], pick[:, q, :], e[:, half], start=True, stop=True
                 )
             prod = work.tile([D, P_NODES, NEI], F32, name="prod")
             nc.vector.tensor_tensor(prod[:], e_all[:], feat_sb[:], op=ALU.mult)
             nc.vector.tensor_reduce(vsum[:, r * P_NODES : (r + 1) * P_NODES], prod[:], axis=X, op=ALU.add)
-        rsum_own = held.tile([128, GROUPS, G_NODES], F32, name="rsum_own")
+
+        esum = held.tile([128, HALVES, G_NODES], F32, name="esum")
+        nc.vector.tensor_reduce(esum[:], e[:], axis=X, op=ALU.add)
+        rsum = held.tile([128, HALVES, G_NODES], F32, name="rsum")
+        nc.vector.reciprocal(rsum[:], esum[:])
+        rsum_own = held.tile([128, HALVES, QUADS, G_NODES], F32, name="rsum_own")
         nc.vector.tensor_tensor(
             rsum_own[:],
-            rsum[:].unsqueeze(1).to_broadcast([128, GROUPS, G_NODES]),
-            first_of_group.to_broadcast([128, GROUPS, G_NODES]),
+            rsum[:].unsqueeze(2).to_broadcast([128, HALVES, QUADS, G_NODES]),
+            first_of_quad.unsqueeze(1).to_broadcast([128, HALVES, QUADS, G_NODES]),
             op=ALU.mult,
         )
-        rsum_all = psum.tile([D, NODES], F32, name="rsum_all")
-        nc.tensor.matmul(rsum_all[:], ones[:], rsum_own[:].rearrange("k g n -> k (g n)"), start=True, stop=True)
+        rsum_all = psum_score.tile([D, NODES], F32, name="rsum_all", tag="score")
+        nc.tensor.matmul(rsum_all[:], ones[:], rsum_own[:].rearrange("k h q n -> k (h q n)"), start=True, stop=True)
 
         v = held.tile([D, NODES], F32, name="v")
         nc.vector.tensor_tensor(v[:], rsum_all[:], vsum[:], op=ALU.mult)

@@ -37,9 +37,8 @@ def tile_sc_encoder_kernel(tc, table, h_ref, a_nei, a_ref, offs, out):
     with (
         tc.tile_pool(name="held", bufs=1) as held,
         tc.tile_pool(name="work", bufs=2) as work,
-        tc.psum_pool(name="psum_score", bufs=HALVES) as psum_score,
         tc.psum_pool(name="psum_feat", bufs=PIECES) as psum_feat,
-        tc.psum_pool(name="psum_spread", bufs=2) as psum_spread,
+        tc.psum_pool(name="psum_turn", bufs=8 - PIECES) as psum_turn,
     ):
         zeros = held.tile([128, 128], BF16, name="zeros")
         nc.gpsimd.memset(zeros[:], 0.0)
@@ -72,13 +71,13 @@ def tile_sc_encoder_kernel(tc, table, h_ref, a_nei, a_ref, offs, out):
         w_nei = held.tile([D, QUADS, 128], BF16, name="w_nei")
         nc.vector.tensor_scalar_mul(w_nei[:], in_quad[:], anei_sb[:, 0:1])
 
-        warm = psum_spread.tile([128, PIECE // 128, 128], F32, name="warm", tag="e_all")
+        warm = psum_turn.tile([128, PIECE // 128, 128], F32, name="warm", tag="bank")
         for i in range(WARM_UP):
             nc.tensor.matmul(
                 warm[:], zeros[:], zeros[:].unsqueeze(1).to_broadcast([128, PIECE // 128, 128]), start=True, stop=True
             )
 
-        s_ref_ps = psum_spread.tile([128, HALVES, G_NODES], F32, name="s_ref_ps", tag="e_all")
+        s_ref_ps = psum_turn.tile([128, HALVES, G_NODES], F32, name="s_ref_ps", tag="bank")
         for half in range(HALVES):
             for q in range(QUADS):
                 group = half * QUADS + q
@@ -91,7 +90,7 @@ def tile_sc_encoder_kernel(tc, table, h_ref, a_nei, a_ref, offs, out):
                 )
         s_ref = held.tile([128, HALVES, G_NODES], F32, name="s_ref")
         nc.scalar.copy(s_ref[:], s_ref_ps[:])
-        s_nei = [psum_score.tile([128, G_NODES, NEI], F32, name=f"s_nei{half}", tag="score") for half in range(HALVES)]
+        s_nei = [psum_turn.tile([128, G_NODES, NEI], F32, name=f"s_nei{half}", tag="bank") for half in range(HALVES)]
         for half in range(HALVES):
             for q in range(QUADS):
                 group = half * QUADS + q
@@ -118,13 +117,10 @@ def tile_sc_encoder_kernel(tc, table, h_ref, a_nei, a_ref, offs, out):
             nc.vector.tensor_tensor(
                 score[:], s_nei[half][:], s_ref[:, half].unsqueeze(2).to_broadcast([128, G_NODES, NEI]), op=ALU.add
             )
-            top_score = work.tile([128, G_NODES], F32, name="top_score")
-            nc.vector.tensor_reduce(top_score[:], s_nei[half][:], axis=X, op=ALU.max)
             act = work.tile([128, G_NODES, NEI], F32, name="act")
             nc.vector.scalar_tensor_tensor(act[:], score[:], SLOPE, score[:], op0=ALU.mult, op1=ALU.max)
-            nc.vector.tensor_tensor(top_score[:], top_score[:], s_ref[:, half], op=ALU.add)
             top = work.tile([128, G_NODES], F32, name="top")
-            nc.vector.scalar_tensor_tensor(top[:], top_score[:], SLOPE, top_score[:], op0=ALU.mult, op1=ALU.max)
+            nc.vector.tensor_reduce(top[:], act[:], axis=X, op=ALU.max)
             shifted = work.tile([128, G_NODES, NEI], F32, name="shifted")
             nc.vector.tensor_tensor(
                 shifted[:], act[:], top[:].unsqueeze(2).to_broadcast([128, G_NODES, NEI]), op=ALU.subtract
@@ -135,7 +131,7 @@ def tile_sc_encoder_kernel(tc, table, h_ref, a_nei, a_ref, offs, out):
         for r in range(PIECES):
             feat_sb = held.tile([D, P_NODES, NEI], F32, name=f"feat_sb{r}")
             nc.scalar.copy(feat_sb[:], feats[r][:])
-            e_all = psum_spread.tile([D, P_NODES, NEI], F32, name="e_all", tag="e_all")
+            e_all = psum_turn.tile([D, P_NODES, NEI], F32, name="e_all", tag="bank")
             for k in range(P_GROUPS):
                 half, q = divmod(r * P_GROUPS + k, QUADS)
                 nc.tensor.matmul(
@@ -156,7 +152,7 @@ def tile_sc_encoder_kernel(tc, table, h_ref, a_nei, a_ref, offs, out):
             first_of_quad.unsqueeze(1).to_broadcast([128, HALVES, QUADS, G_NODES]),
             op=ALU.mult,
         )
-        rsum_all = psum_score.tile([D, NODES], F32, name="rsum_all", tag="score")
+        rsum_all = psum_turn.tile([D, NODES], F32, name="rsum_all", tag="bank")
         nc.tensor.matmul(rsum_all[:], ones[:], rsum_own[:].rearrange("k h q n -> k (h q n)"), start=True, stop=True)
 
         v = held.tile([D, NODES], F32, name="v")

@@ -27,8 +27,6 @@ P_NODES = PIECE // NEI
 P_COLS = PIECE // 16
 P_GROUPS = P_NODES // G_NODES
 
-WARM_UP = 4
-
 FLOPS = 2 * D * N + 2 * D * NODES + 2 * D * N
 
 
@@ -40,9 +38,6 @@ def tile_sc_encoder_kernel(tc, table, h_ref, a_nei, a_ref, offs, out):
         tc.psum_pool(name="psum_feat", bufs=PIECES) as psum_feat,
         tc.psum_pool(name="psum_turn", bufs=8 - PIECES) as psum_turn,
     ):
-        zeros = held.tile([128, 128], BF16, name="zeros")
-        nc.gpsimd.memset(zeros[:], 0.0)
-
         aref_sb = held.tile([D, 1], BF16, name="aref_sb")
         nc.sync.dma_start(aref_sb[:], a_ref)
         anei_sb = held.tile([D, 1], BF16, name="anei_sb")
@@ -70,12 +65,6 @@ def tile_sc_encoder_kernel(tc, table, h_ref, a_nei, a_ref, offs, out):
         nc.vector.tensor_scalar_mul(w_ref[:], in_quad[:], aref_sb[:, 0:1])
         w_nei = held.tile([D, QUADS, 128], BF16, name="w_nei")
         nc.vector.tensor_scalar_mul(w_nei[:], in_quad[:], anei_sb[:, 0:1])
-
-        warm = psum_turn.tile([128, PIECE // 128, 128], F32, name="warm", tag="bank")
-        for i in range(WARM_UP):
-            nc.tensor.matmul(
-                warm[:], zeros[:], zeros[:].unsqueeze(1).to_broadcast([128, PIECE // 128, 128]), start=True, stop=True
-            )
 
         s_ref_ps = psum_turn.tile([128, HALVES, G_NODES], F32, name="s_ref_ps", tag="bank")
         for half in range(HALVES):

@@ -144,12 +144,12 @@ def tile_sc_encoder_kernel(tc, table, h_ref, a_nei, a_ref, offs, out):
         rsum_all = psum_turn.tile([D, NODES], F32, name="rsum_all", tag="bank")
         nc.tensor.matmul(rsum_all[:], ones[:], rsum_own[:].rearrange("k h q n -> k (h q n)"), start=True, stop=True)
 
-        v = held.tile([D, NODES], F32, name="v")
-        nc.vector.tensor_tensor(v[:], rsum_all[:], vsum[:], op=ALU.mult)
-        exp_v = held.tile([D, NODES], F32, name="exp_v")
-        nc.scalar.activation(exp_v[:], v[:], ACT.Exp)
+        neg = held.tile([D, NODES], F32, name="neg")
+        nc.vector.scalar_tensor_tensor(neg[:], vsum[:], 0.0, rsum_all[:], op0=ALU.min, op1=ALU.mult)
+        exp_neg = held.tile([D, NODES], F32, name="exp_neg")
+        nc.scalar.activation(exp_neg[:], neg[:], ACT.Exp)
         pos = held.tile([D, NODES], F32, name="pos")
-        nc.vector.tensor_scalar(pos[:], v[:], 0.0, -1.0, op0=ALU.max, op1=ALU.add)
+        nc.vector.scalar_tensor_tensor(pos[:], vsum[:], 0.0, rsum_all[:], op0=ALU.max, op1=ALU.mult)
         res = held.tile([D, NODES], F32, name="res")
-        nc.vector.scalar_tensor_tensor(res[:], exp_v[:], 1.0, pos[:], op0=ALU.min, op1=ALU.add)
+        nc.vector.scalar_tensor_tensor(res[:], pos[:], -1.0, exp_neg[:], op0=ALU.add, op1=ALU.add)
         nc.sync.dma_start(out, res[:])

@@ -15,17 +15,23 @@ NEI = 16
 N = NODES * NEI
 SLOPE = 0.01
 
-HALVES = 2
-QUADS = 4
-Q_PARTS = 128 // QUADS
-G_NODES = NODES // (HALVES * QUADS)
+GROUPS = 8
+G_PARTS = 128 // GROUPS
+G_NODES = NODES // GROUPS
 G_COLS = G_NODES * NEI // 16
 
 PIECE = 512
 PIECES = N // PIECE
-P_NODES = PIECE // NEI
 P_COLS = PIECE // 16
-P_GROUPS = P_NODES // G_NODES
+
+CHUNK = 128
+CHUNKS = N // CHUNK
+C_NODES = CHUNK // NEI
+G_CHUNKS = CHUNKS // GROUPS
+P_CHUNKS = PIECE // CHUNK
+SUMMANDS = 3
+
+PSUM_BANKS = 8
 
 FLOPS = 2 * D * N + 2 * D * NODES + 2 * D * N
 
@@ -34,9 +40,7 @@ def tile_sc_encoder_kernel(tc, table, h_ref, a_nei, a_ref, offs, out):
     nc = tc.nc
     with (
         tc.tile_pool(name="held", bufs=1) as held,
-        tc.tile_pool(name="work", bufs=2) as work,
-        tc.psum_pool(name="psum_feat", bufs=PIECES) as psum_feat,
-        tc.psum_pool(name="psum_turn", bufs=8 - PIECES) as psum_turn,
+        tc.psum_pool(name="psum", bufs=PSUM_BANKS) as psum,
     ):
         aref_sb = held.tile([D, 1], BF16, name="aref_sb")
         nc.sync.dma_start(aref_sb[:], a_ref)
@@ -49,107 +53,130 @@ def tile_sc_encoder_kernel(tc, table, h_ref, a_nei, a_ref, offs, out):
         offsets = held.tile([128, N // 16], U16, name="offsets")
         nc.sync.dma_start(offsets[:], offs)
 
-        in_quad = held.tile([D, QUADS, 128], BF16, name="in_quad")
-        nc.vector.memset(in_quad[:], 0.0)
-        for q in range(QUADS):
-            nc.vector.memset(in_quad[:, q, q * Q_PARTS : (q + 1) * Q_PARTS], 1.0)
-        ident = held.tile([D, D], BF16, name="ident")
+        in_block = held.tile([D, GROUPS, 128], BF16, name="in_block")
+        nc.vector.memset(in_block[:], 0.0)
+        for g in range(GROUPS):
+            nc.vector.memset(in_block[:, g, g * G_PARTS : (g + 1) * G_PARTS], 1.0)
+        ident = held.tile([128, 128], BF16, name="ident")
         make_identity(nc, ident[:])
-        first_of_quad = ident[:].rearrange("k (q i) -> k q i", i=Q_PARTS)[:, :, 0:1]
-        pick = held.tile([128, QUADS, D], F32, name="pick")
-        nc.gpsimd.tensor_copy(pick[:], first_of_quad.to_broadcast([128, QUADS, D]))
-        ones = held.tile([128, D], F32, name="ones")
+        ident_f32 = held.tile([128, 128], F32, name="ident_f32")
+        make_identity(nc, ident_f32[:])
+        ones = held.tile([CHUNK, D], BF16, name="ones")
         nc.gpsimd.memset(ones[:], 1.0)
 
-        w_ref = held.tile([D, QUADS, 128], BF16, name="w_ref")
-        nc.vector.tensor_scalar_mul(w_ref[:], in_quad[:], aref_sb[:, 0:1])
-        w_nei = held.tile([D, QUADS, 128], BF16, name="w_nei")
-        nc.vector.tensor_scalar_mul(w_nei[:], in_quad[:], anei_sb[:, 0:1])
+        w_ref = held.tile([D, GROUPS, 128], BF16, name="w_ref")
+        nc.vector.tensor_scalar_mul(w_ref[:], in_block[:], aref_sb[:, 0:1])
+        w_nei = held.tile([D, GROUPS, 128], BF16, name="w_nei")
+        nc.vector.tensor_scalar_mul(w_nei[:], in_block[:], anei_sb[:, 0:1])
+        own_node = held.tile([CHUNK, C_NODES], F32, name="own_node")
+        nc.vector.tensor_reduce(own_node[:], ident[:].rearrange("j (n t) -> j n t", t=NEI), axis=X, op=ALU.add)
 
-        s_ref_ps = psum_turn.tile([128, HALVES, G_NODES], F32, name="s_ref_ps", tag="bank")
-        for half in range(HALVES):
-            for q in range(QUADS):
-                group = half * QUADS + q
-                nc.tensor.matmul(
-                    s_ref_ps[:, half, :],
-                    w_ref[:, q, :],
-                    href_sb[:, group * G_NODES : (group + 1) * G_NODES],
-                    start=(q == 0),
-                    stop=(q == QUADS - 1),
-                )
-        s_ref = held.tile([128, HALVES, G_NODES], F32, name="s_ref")
+        s_ref_ps = psum.tile([128, G_NODES], F32, name="s_ref_ps", tag="bank")
+        for g in range(GROUPS):
+            nc.tensor.matmul(
+                s_ref_ps[:],
+                w_ref[:, g, :],
+                href_sb[:, g * G_NODES : (g + 1) * G_NODES],
+                start=(g == 0),
+                stop=(g == GROUPS - 1),
+            )
+        s_ref = held.tile([128, G_NODES], F32, name="s_ref")
         nc.scalar.copy(s_ref[:], s_ref_ps[:])
-        s_nei = [psum_turn.tile([128, G_NODES, NEI], F32, name=f"s_nei{half}", tag="bank") for half in range(HALVES)]
-        for half in range(HALVES):
-            for q in range(QUADS):
-                group = half * QUADS + q
-                nc.tensor.matmul(
-                    s_nei[half][:].rearrange("p n t -> p (n t)"),
-                    w_nei[:, q, :],
-                    table_sb[:].indirect(offsets[:, group * G_COLS : (group + 1) * G_COLS]),
-                    start=(q == 0),
-                    stop=(q == QUADS - 1),
-                )
-        feats = [psum_feat.tile([D, P_NODES, NEI], F32, name=f"feat{r}", tag="feat") for r in range(PIECES)]
+        s_nei = psum.tile([128, G_NODES, NEI], F32, name="s_nei", tag="bank")
+        for g in range(GROUPS):
+            nc.tensor.matmul(
+                s_nei[:].rearrange("p n t -> p (n t)"),
+                w_nei[:, g, :],
+                table_sb[:].indirect(offsets[:, g * G_COLS : (g + 1) * G_COLS]),
+                start=(g == 0),
+                stop=(g == GROUPS - 1),
+            )
+        feats = [psum.tile([D, PIECE], F32, name=f"feat{r}", tag="bank") for r in range(PIECES)]
         for r in range(PIECES):
             nc.tensor.matmul(
-                feats[r][:].rearrange("p n t -> p (n t)"),
+                feats[r][:],
                 ident[:],
                 table_sb[:].indirect(offsets[:, r * P_COLS : (r + 1) * P_COLS]),
                 start=True,
                 stop=True,
             )
 
-        e = held.tile([128, HALVES, G_NODES, NEI], F32, name="e")
-        for half in range(HALVES):
-            score = work.tile([128, G_NODES, NEI], F32, name="score")
-            nc.vector.tensor_tensor(
-                score[:], s_nei[half][:], s_ref[:, half].unsqueeze(2).to_broadcast([128, G_NODES, NEI]), op=ALU.add
-            )
-            act = work.tile([128, G_NODES, NEI], F32, name="act")
-            nc.vector.scalar_tensor_tensor(act[:], score[:], SLOPE, score[:], op0=ALU.mult, op1=ALU.max)
-            top = work.tile([128, G_NODES], F32, name="top")
-            nc.vector.tensor_reduce(top[:], act[:], axis=X, op=ALU.max)
-            shifted = work.tile([128, G_NODES, NEI], F32, name="shifted")
-            nc.vector.tensor_tensor(
-                shifted[:], act[:], top[:].unsqueeze(2).to_broadcast([128, G_NODES, NEI]), op=ALU.subtract
-            )
-            nc.scalar.activation(e[:, half], shifted[:], ACT.Exp)
+        over_t = [128, G_NODES, NEI]
+        score = held.tile(over_t, F32, name="score")
+        nc.vector.tensor_tensor(score[:], s_nei[:], s_ref[:].unsqueeze(2).to_broadcast(over_t), op=ALU.add)
+        act = held.tile(over_t, F32, name="act")
+        nc.vector.scalar_tensor_tensor(act[:], score[:], SLOPE, score[:], op0=ALU.mult, op1=ALU.max)
+        top = held.tile([128, G_NODES], F32, name="top")
+        nc.vector.tensor_reduce(top[:], act[:], axis=X, op=ALU.max)
+        shifted = held.tile(over_t, F32, name="shifted")
+        nc.vector.tensor_tensor(shifted[:], act[:], top[:].unsqueeze(2).to_broadcast(over_t), op=ALU.subtract)
+        e = held.tile([128, G_CHUNKS, CHUNK], F32, name="e")
+        nc.scalar.activation(e[:].rearrange("p u j -> p (u j)"), shifted[:].rearrange("p n t -> p (n t)"), ACT.Exp)
 
-        vsum = held.tile([D, NODES], F32, name="vsum")
-        for r in range(PIECES):
-            feat_sb = held.tile([D, P_NODES, NEI], F32, name=f"feat_sb{r}")
-            nc.scalar.copy(feat_sb[:], feats[r][:])
-            e_all = psum_turn.tile([D, P_NODES, NEI], F32, name="e_all", tag="bank")
-            for k in range(P_GROUPS):
-                half, q = divmod(r * P_GROUPS + k, QUADS)
-                nc.tensor.matmul(
-                    e_all[:, k * G_NODES : (k + 1) * G_NODES, :], pick[:, q, :], e[:, half], start=True, stop=True
-                )
-            prod = work.tile([D, P_NODES, NEI], F32, name="prod")
-            nc.vector.tensor_tensor(prod[:], e_all[:], feat_sb[:], op=ALU.mult)
-            nc.vector.tensor_reduce(vsum[:, r * P_NODES : (r + 1) * P_NODES], prod[:], axis=X, op=ALU.add)
-
-        esum = held.tile([128, HALVES, G_NODES], F32, name="esum")
-        nc.vector.tensor_reduce(esum[:], e[:], axis=X, op=ALU.add)
-        rsum = held.tile([128, HALVES, G_NODES], F32, name="rsum")
-        nc.vector.reciprocal(rsum[:], esum[:])
-        rsum_own = held.tile([128, HALVES, QUADS, G_NODES], F32, name="rsum_own")
+        e_flip = psum.tile([CHUNK, G_CHUNKS, 128], F32, name="e_flip", tag="bank")
+        for u in range(G_CHUNKS):
+            nc.tensor.transpose(e_flip[:, u, :], e[:, u, :], ident_f32[:])
+        rest = held.tile([CHUNK, CHUNKS, SUMMANDS], F32, name="rest")
+        upper = rest[:].bitcast(BF16).rearrange("j c (s half) -> j c s half", half=2)[:, :, :, 1]
+        nc.vector.tensor_copy(
+            rest[:].rearrange("j (g u) s -> j g u s", u=G_CHUNKS)[:, :, :, 0],
+            e_flip[:].rearrange("j u (g i) -> j g u i", i=G_PARTS)[:, :, :, 0],
+        )
+        for s in range(SUMMANDS - 1):
+            nc.vector.tensor_tensor(rest[:, :, s + 1], rest[:, :, s], upper[:, :, s], op=ALU.subtract)
+        cols = [CHUNK, CHUNKS, SUMMANDS, C_NODES]
+        e_cols = held.tile(cols, BF16, name="e_cols")
         nc.vector.tensor_tensor(
-            rsum_own[:],
-            rsum[:].unsqueeze(2).to_broadcast([128, HALVES, QUADS, G_NODES]),
-            first_of_quad.unsqueeze(1).to_broadcast([128, HALVES, QUADS, G_NODES]),
+            e_cols[:],
+            upper.unsqueeze(3).to_broadcast(cols),
+            own_node[:].unsqueeze(1).unsqueeze(1).to_broadcast(cols),
             op=ALU.mult,
         )
-        rsum_all = psum_turn.tile([D, NODES], F32, name="rsum_all", tag="bank")
-        nc.tensor.matmul(rsum_all[:], ones[:], rsum_own[:].rearrange("k h q n -> k (h q n)"), start=True, stop=True)
+
+        feat_flip = []
+        for r in range(PIECES):
+            feat_sb = held.tile([D, P_CHUNKS, CHUNK], BF16, name=f"feat_sb{r}")
+            nc.scalar.copy(feat_sb[:].rearrange("d k j -> d (k j)"), feats[r][:])
+            flip_ps = psum.tile([CHUNK, P_CHUNKS, D], BF16, name=f"flip_ps{r}", tag="bank")
+            for k in range(P_CHUNKS):
+                nc.tensor.transpose(flip_ps[:, k, :], feat_sb[:, k, :], ident[:])
+            flipped = held.tile([CHUNK, P_CHUNKS, D], BF16, name=f"feat_flip{r}")
+            nc.vector.tensor_copy(flipped[:], flip_ps[:])
+            feat_flip.append(flipped)
+
+        esum_ps = psum.tile([D, CHUNKS, SUMMANDS, C_NODES], F32, name="esum_ps", tag="bank")
+        nc.tensor.matmul(
+            esum_ps[:].rearrange("d c s n -> d (c s n)"),
+            ones[:],
+            e_cols[:].rearrange("j c s n -> j (c s n)"),
+            start=True,
+            stop=True,
+        )
+        esum = held.tile([D, CHUNKS, C_NODES], F32, name="esum")
+        nc.vector.tensor_reduce(esum[:], esum_ps[:].rearrange("d c s n -> d c n s"), axis=X, op=ALU.add)
+        rsum = held.tile([D, NODES], F32, name="rsum")
+        nc.vector.reciprocal(rsum[:], esum[:].rearrange("d c n -> d (c n)"))
+
+        vsum_ps = psum.tile([D, CHUNKS, SUMMANDS, C_NODES], F32, name="vsum_ps", tag="bank")
+        for c in range(CHUNKS):
+            r, k = divmod(c, P_CHUNKS)
+            nc.tensor.matmul(
+                vsum_ps[:, c].rearrange("d s n -> d (s n)"),
+                feat_flip[r][:, k, :],
+                e_cols[:, c].rearrange("j s n -> j (s n)"),
+                start=True,
+                stop=True,
+            )
+        vsum = held.tile([D, CHUNKS, C_NODES], F32, name="vsum")
+        nc.vector.tensor_reduce(vsum[:], vsum_ps[:].rearrange("d c s n -> d c n s"), axis=X, op=ALU.add)
+        vsum_flat = vsum[:].rearrange("d c n -> d (c n)")
 
         neg = held.tile([D, NODES], F32, name="neg")
-        nc.vector.scalar_tensor_tensor(neg[:], vsum[:], 0.0, rsum_all[:], op0=ALU.min, op1=ALU.mult)
+        nc.vector.scalar_tensor_tensor(neg[:], vsum_flat, 0.0, rsum[:], op0=ALU.min, op1=ALU.mult)
         exp_neg = held.tile([D, NODES], F32, name="exp_neg")
         nc.scalar.activation(exp_neg[:], neg[:], ACT.Exp)
         pos = held.tile([D, NODES], F32, name="pos")
-        nc.vector.scalar_tensor_tensor(pos[:], vsum[:], 0.0, rsum_all[:], op0=ALU.max, op1=ALU.mult)
+        nc.vector.scalar_tensor_tensor(pos[:], vsum_flat, 0.0, rsum[:], op0=ALU.max, op1=ALU.mult)
         res = held.tile([D, NODES], F32, name="res")
         nc.vector.scalar_tensor_tensor(res[:], pos[:], -1.0, exp_neg[:], op0=ALU.add, op1=ALU.add)
         nc.sync.dma_start(out, res[:])

@@ -14,11 +14,12 @@ NODES = 128
 NEI = 16
 N = NODES * NEI
 SLOPE = 0.01
+FAR = 2.0**126
 
 GROUPS = 8
-G_PARTS = 128 // GROUPS
 G_NODES = NODES // GROUPS
-G_COLS = G_NODES * NEI // 16
+G_ENTRIES = G_NODES * NEI
+G_COLS = G_ENTRIES // 16
 
 PIECE = 512
 PIECES = N // PIECE
@@ -53,42 +54,33 @@ def tile_sc_encoder_kernel(tc, table, h_ref, a_nei, a_ref, offs, out):
         offsets = held.tile([128, N // 16], U16, name="offsets")
         nc.sync.dma_start(offsets[:], offs)
 
-        in_block = held.tile([D, GROUPS, 128], BF16, name="in_block")
-        nc.vector.memset(in_block[:], 0.0)
+        in_group = held.tile([D, GROUPS, NODES], BF16, name="in_group")
+        nc.vector.memset(in_group[:], 0.0)
         for g in range(GROUPS):
-            nc.vector.memset(in_block[:, g, g * G_PARTS : (g + 1) * G_PARTS], 1.0)
+            nc.vector.memset(in_group[:, g, g * G_NODES : (g + 1) * G_NODES], 1.0)
         ident = held.tile([128, 128], BF16, name="ident")
         make_identity(nc, ident[:])
         ident_f32 = held.tile([128, 128], F32, name="ident_f32")
         make_identity(nc, ident_f32[:])
-        ones = held.tile([CHUNK, D], BF16, name="ones")
-        nc.gpsimd.memset(ones[:], 1.0)
+        own = held.tile([NODES, G_NODES], F32, name="own")
+        nc.vector.tensor_reduce(own[:], ident[:].rearrange("p (g n) -> p n g", n=G_NODES), axis=X, op=ALU.add)
+        others = held.tile([NODES, G_NODES], BF16, name="others")
+        nc.vector.tensor_scalar(others[:], own[:], -1.0, FAR, op0=ALU.add, op1=ALU.mult)
+        w_nei = held.tile([D, GROUPS, NODES], BF16, name="w_nei")
+        nc.vector.tensor_scalar_mul(w_nei[:], in_group[:], anei_sb[:, 0:1])
 
-        w_ref = held.tile([D, GROUPS, 128], BF16, name="w_ref")
-        nc.vector.tensor_scalar_mul(w_ref[:], in_block[:], aref_sb[:, 0:1])
-        w_nei = held.tile([D, GROUPS, 128], BF16, name="w_nei")
-        nc.vector.tensor_scalar_mul(w_nei[:], in_block[:], anei_sb[:, 0:1])
-        own_node = held.tile([CHUNK, C_NODES], F32, name="own_node")
-        nc.vector.tensor_reduce(own_node[:], ident[:].rearrange("j (n t) -> j n t", t=NEI), axis=X, op=ALU.add)
-
-        s_ref_ps = psum.tile([128, G_NODES], F32, name="s_ref_ps", tag="bank")
+        score = psum.tile([NODES, G_NODES, NEI], F32, name="score", tag="bank")
+        score_flat = score[:].rearrange("p n t -> p (n t)")
+        nc.tensor.matmul(
+            score[:], ident[:], others[:].unsqueeze(2).to_broadcast([NODES, G_NODES, NEI]), start=True, stop=False
+        )
+        nc.tensor.matmul(score_flat, href_sb[:], aref_sb[:, 0:1].to_broadcast([D, G_ENTRIES]), start=False, stop=False)
         for g in range(GROUPS):
             nc.tensor.matmul(
-                s_ref_ps[:],
-                w_ref[:, g, :],
-                href_sb[:, g * G_NODES : (g + 1) * G_NODES],
-                start=(g == 0),
-                stop=(g == GROUPS - 1),
-            )
-        s_ref = held.tile([128, G_NODES], F32, name="s_ref")
-        nc.scalar.copy(s_ref[:], s_ref_ps[:])
-        s_nei = psum.tile([128, G_NODES, NEI], F32, name="s_nei", tag="bank")
-        for g in range(GROUPS):
-            nc.tensor.matmul(
-                s_nei[:].rearrange("p n t -> p (n t)"),
+                score_flat,
                 w_nei[:, g, :],
                 table_sb[:].indirect(offsets[:, g * G_COLS : (g + 1) * G_COLS]),
-                start=(g == 0),
+                start=False,
                 stop=(g == GROUPS - 1),
             )
         feats = [psum.tile([D, PIECE], F32, name=f"feat{r}", tag="bank") for r in range(PIECES)]
@@ -101,37 +93,34 @@ def tile_sc_encoder_kernel(tc, table, h_ref, a_nei, a_ref, offs, out):
                 stop=True,
             )
 
-        over_t = [128, G_NODES, NEI]
-        score = held.tile(over_t, F32, name="score")
-        nc.vector.tensor_tensor(score[:], s_nei[:], s_ref[:].unsqueeze(2).to_broadcast(over_t), op=ALU.add)
-        act = held.tile(over_t, F32, name="act")
-        nc.vector.scalar_tensor_tensor(act[:], score[:], SLOPE, score[:], op0=ALU.mult, op1=ALU.max)
-        top = held.tile([128, G_NODES], F32, name="top")
-        nc.vector.tensor_reduce(top[:], act[:], axis=X, op=ALU.max)
-        shifted = held.tile(over_t, F32, name="shifted")
-        nc.vector.tensor_tensor(shifted[:], act[:], top[:].unsqueeze(2).to_broadcast(over_t), op=ALU.subtract)
-        e = held.tile([128, G_CHUNKS, CHUNK], F32, name="e")
-        nc.scalar.activation(e[:].rearrange("p u j -> p (u j)"), shifted[:].rearrange("p n t -> p (n t)"), ACT.Exp)
+        minus_score = held.tile([NODES, G_ENTRIES], F32, name="minus_score")
+        minus_max = held.tile([NODES, 1], F32, name="minus_max")
+        nc.vector.tensor_scalar(
+            minus_score[:], score_flat, -1.0, None, op0=ALU.mult, op1=ALU.min, accum_out=minus_max[:]
+        )
+        minus_act = held.tile([NODES, G_ENTRIES], F32, name="minus_act")
+        nc.vector.scalar_tensor_tensor(minus_act[:], minus_score[:], SLOPE, minus_score[:], op0=ALU.mult, op1=ALU.min)
+        minus_top = held.tile([NODES, 1], F32, name="minus_top")
+        nc.vector.scalar_tensor_tensor(minus_top[:], minus_max[:], SLOPE, minus_max[:], op0=ALU.mult, op1=ALU.min)
+        e = held.tile([NODES, G_ENTRIES], F32, name="e")
+        esum = held.tile([NODES, 1], F32, name="esum")
+        nc.scalar.activation(e[:], minus_act[:], ACT.Exp, bias=minus_top[:], scale=-1.0, accum_out=esum[:])
+        rsum = held.tile([NODES, 1], F32, name="rsum")
+        nc.vector.reciprocal(rsum[:], esum[:])
+        att = held.tile([NODES, G_CHUNKS, CHUNK], F32, name="att")
+        nc.vector.tensor_scalar_mul(att[:].rearrange("p h j -> p (h j)"), e[:], rsum[:, 0:1])
 
-        e_flip = psum.tile([CHUNK, G_CHUNKS, 128], F32, name="e_flip", tag="bank")
-        for u in range(G_CHUNKS):
-            nc.tensor.transpose(e_flip[:, u, :], e[:, u, :], ident_f32[:])
-        rest = held.tile([CHUNK, CHUNKS, SUMMANDS], F32, name="rest")
-        upper = rest[:].bitcast(BF16).rearrange("j c (s half) -> j c s half", half=2)[:, :, :, 1]
-        nc.vector.tensor_copy(
-            rest[:].rearrange("j (g u) s -> j g u s", u=G_CHUNKS)[:, :, :, 0],
-            e_flip[:].rearrange("j u (g i) -> j g u i", i=G_PARTS)[:, :, :, 0],
-        )
+        att_flip = psum.tile([CHUNK, G_CHUNKS, NODES], F32, name="att_flip", tag="bank")
+        rest = held.tile([CHUNK, SUMMANDS, NODES], F32, name="rest")
+        for h in range(G_CHUNKS):
+            nc.tensor.transpose(att_flip[:, h, :], att[:, h, :], ident_f32[:])
+            nc.vector.tensor_copy(
+                rest[:, 0, :].rearrange("j (g h n) -> j g h n", h=G_CHUNKS, n=C_NODES)[:, :, h, :],
+                att_flip[:, h, :].rearrange("j (g h n) -> j g h n", h=G_CHUNKS, n=C_NODES)[:, :, h, :],
+            )
+        upper = rest[:].bitcast(BF16).rearrange("j s (p half) -> j s p half", half=2)[:, :, :, 1]
         for s in range(SUMMANDS - 1):
-            nc.vector.tensor_tensor(rest[:, :, s + 1], rest[:, :, s], upper[:, :, s], op=ALU.subtract)
-        cols = [CHUNK, CHUNKS, SUMMANDS, C_NODES]
-        e_cols = held.tile(cols, BF16, name="e_cols")
-        nc.vector.tensor_tensor(
-            e_cols[:],
-            upper.unsqueeze(3).to_broadcast(cols),
-            own_node[:].unsqueeze(1).unsqueeze(1).to_broadcast(cols),
-            op=ALU.mult,
-        )
+            nc.vector.tensor_tensor(rest[:, s + 1, :], rest[:, s, :], upper[:, s, :], op=ALU.subtract)
 
         feat_flip = []
         for r in range(PIECES):
@@ -144,39 +133,20 @@ def tile_sc_encoder_kernel(tc, table, h_ref, a_nei, a_ref, offs, out):
             nc.vector.tensor_copy(flipped[:], flip_ps[:])
             feat_flip.append(flipped)
 
-        esum_ps = psum.tile([D, CHUNKS, SUMMANDS, C_NODES], F32, name="esum_ps", tag="bank")
-        nc.tensor.matmul(
-            esum_ps[:].rearrange("d c s n -> d (c s n)"),
-            ones[:],
-            e_cols[:].rearrange("j c s n -> j (c s n)"),
-            start=True,
-            stop=True,
-        )
-        esum = held.tile([D, CHUNKS, C_NODES], F32, name="esum")
-        nc.vector.tensor_reduce(esum[:], esum_ps[:].rearrange("d c s n -> d c n s"), axis=X, op=ALU.add)
-        rsum = held.tile([D, NODES], F32, name="rsum")
-        nc.vector.reciprocal(rsum[:], esum[:].rearrange("d c n -> d (c n)"))
-
-        vsum_ps = psum.tile([D, CHUNKS, SUMMANDS, C_NODES], F32, name="vsum_ps", tag="bank")
+        v_parts = psum.tile([D, SUMMANDS, NODES], F32, name="v_parts", tag="bank")
         for c in range(CHUNKS):
             r, k = divmod(c, P_CHUNKS)
-            nc.tensor.matmul(
-                vsum_ps[:, c].rearrange("d s n -> d (s n)"),
-                feat_flip[r][:, k, :],
-                e_cols[:, c].rearrange("j s n -> j (s n)"),
-                start=True,
-                stop=True,
-            )
-        vsum = held.tile([D, CHUNKS, C_NODES], F32, name="vsum")
-        nc.vector.tensor_reduce(vsum[:], vsum_ps[:].rearrange("d c s n -> d c n s"), axis=X, op=ALU.add)
-        vsum_flat = vsum[:].rearrange("d c n -> d (c n)")
+            nodes = slice(c * C_NODES, (c + 1) * C_NODES)
+            nc.tensor.matmul(v_parts[:, :, nodes], feat_flip[r][:, k, :], upper[:, :, nodes], start=True, stop=True)
+        v = held.tile([D, NODES], F32, name="v")
+        nc.vector.tensor_reduce(v[:], v_parts[:].rearrange("d s p -> d p s"), axis=X, op=ALU.add)
 
         neg = held.tile([D, NODES], F32, name="neg")
-        nc.vector.scalar_tensor_tensor(neg[:], vsum_flat, 0.0, rsum[:], op0=ALU.min, op1=ALU.mult)
+        nc.vector.tensor_scalar_min(neg[:], v[:], 0.0)
         exp_neg = held.tile([D, NODES], F32, name="exp_neg")
         nc.scalar.activation(exp_neg[:], neg[:], ACT.Exp)
         pos = held.tile([D, NODES], F32, name="pos")
-        nc.vector.scalar_tensor_tensor(pos[:], vsum_flat, 0.0, rsum[:], op0=ALU.max, op1=ALU.mult)
+        nc.vector.tensor_scalar(pos[:], v[:], 0.0, -1.0, op0=ALU.max, op1=ALU.add)
         res = held.tile([D, NODES], F32, name="res")
-        nc.vector.scalar_tensor_tensor(res[:], pos[:], -1.0, exp_neg[:], op0=ALU.add, op1=ALU.add)
+        nc.vector.tensor_tensor(res[:], pos[:], exp_neg[:], op=ALU.add)
         nc.sync.dma_start(out, res[:])

@@ -54,10 +54,6 @@ def tile_sc_encoder_kernel(tc, table, h_ref, a_nei, a_ref, offs, out):
         offsets = held.tile([128, N // 16], U16, name="offsets")
         nc.sync.dma_start(offsets[:], offs)
 
-        in_group = held.tile([D, GROUPS, NODES], BF16, name="in_group")
-        nc.vector.memset(in_group[:], 0.0)
-        for g in range(GROUPS):
-            nc.vector.memset(in_group[:, g, g * G_NODES : (g + 1) * G_NODES], 1.0)
         ident = held.tile([128, 128], BF16, name="ident")
         make_identity(nc, ident[:])
         ident_f32 = held.tile([128, 128], F32, name="ident_f32")
@@ -66,8 +62,12 @@ def tile_sc_encoder_kernel(tc, table, h_ref, a_nei, a_ref, offs, out):
         nc.vector.tensor_reduce(own[:], ident[:].rearrange("p (g n) -> p n g", n=G_NODES), axis=X, op=ALU.add)
         others = held.tile([NODES, G_NODES], BF16, name="others")
         nc.vector.tensor_scalar(others[:], own[:], -1.0, FAR, op0=ALU.add, op1=ALU.mult)
-        w_nei = held.tile([D, GROUPS, NODES], BF16, name="w_nei")
-        nc.vector.tensor_scalar_mul(w_nei[:], in_group[:], anei_sb[:, 0:1])
+        w_nei = held.tile([D, GROUPS * (NODES + G_NODES)], BF16, name="w_nei")
+        nc.vector.memset(w_nei[:], 0.0)
+        nc.vector.tensor_copy(
+            w_nei[:].rearrange("k (g r) -> k g r", g=GROUPS)[:, :, 0:G_NODES],
+            anei_sb[:, 0:1].unsqueeze(2).to_broadcast([D, GROUPS, G_NODES]),
+        )
 
         score = psum.tile([NODES, G_NODES, NEI], F32, name="score", tag="bank")
         score_flat = score[:].rearrange("p n t -> p (n t)")
@@ -78,7 +78,7 @@ def tile_sc_encoder_kernel(tc, table, h_ref, a_nei, a_ref, offs, out):
         for g in range(GROUPS):
             nc.tensor.matmul(
                 score_flat,
-                w_nei[:, g, :],
+                w_nei[:, g * NODES : (g + 1) * NODES],
                 table_sb[:].indirect(offsets[:, g * G_COLS : (g + 1) * G_COLS]),
                 start=False,
                 stop=(g == GROUPS - 1),
@@ -107,20 +107,19 @@ def tile_sc_encoder_kernel(tc, table, h_ref, a_nei, a_ref, offs, out):
         nc.scalar.activation(e[:], minus_act[:], ACT.Exp, bias=minus_top[:], scale=-1.0, accum_out=esum[:])
         rsum = held.tile([NODES, 1], F32, name="rsum")
         nc.vector.reciprocal(rsum[:], esum[:])
-        att = held.tile([NODES, G_CHUNKS, CHUNK], F32, name="att")
-        nc.vector.tensor_scalar_mul(att[:].rearrange("p h j -> p (h j)"), e[:], rsum[:, 0:1])
 
-        att_flip = psum.tile([CHUNK, G_CHUNKS, NODES], F32, name="att_flip", tag="bank")
-        rest = held.tile([CHUNK, SUMMANDS, NODES], F32, name="rest")
+        summands = []
         for h in range(G_CHUNKS):
-            nc.tensor.transpose(att_flip[:, h, :], att[:, h, :], ident_f32[:])
-            nc.vector.tensor_copy(
-                rest[:, 0, :].rearrange("j (g h n) -> j g h n", h=G_CHUNKS, n=C_NODES)[:, :, h, :],
-                att_flip[:, h, :].rearrange("j (g h n) -> j g h n", h=G_CHUNKS, n=C_NODES)[:, :, h, :],
-            )
-        upper = rest[:].bitcast(BF16).rearrange("j s (p half) -> j s p half", half=2)[:, :, :, 1]
-        for s in range(SUMMANDS - 1):
-            nc.vector.tensor_tensor(rest[:, s + 1, :], rest[:, s, :], upper[:, s, :], op=ALU.subtract)
+            att = held.tile([NODES, CHUNK], F32, name=f"att{h}")
+            nc.vector.tensor_scalar_mul(att[:], e[:, h * CHUNK : (h + 1) * CHUNK], rsum[:, 0:1])
+            att_flip = psum.tile([CHUNK, GROUPS, G_CHUNKS, C_NODES], F32, name=f"att_flip{h}", tag="bank")
+            nc.tensor.transpose(att_flip[:].rearrange("j g i n -> j (g i n)"), att[:], ident_f32[:])
+            rest = held.tile([CHUNK, SUMMANDS, GROUPS, C_NODES], F32, name=f"rest{h}")
+            nc.vector.tensor_copy(rest[:, 0], att_flip[:, :, h, :])
+            upper = rest[:].bitcast(BF16).rearrange("j s g (n half) -> j s g n half", half=2)[:, :, :, :, 1]
+            for s in range(SUMMANDS - 1):
+                nc.vector.tensor_tensor(rest[:, s + 1], rest[:, s], upper[:, s], op=ALU.subtract)
+            summands.append(upper)
 
         feat_flip = []
         for r in range(PIECES):
@@ -134,19 +133,21 @@ def tile_sc_encoder_kernel(tc, table, h_ref, a_nei, a_ref, offs, out):
             feat_flip.append(flipped)
 
         v_parts = psum.tile([D, SUMMANDS, NODES], F32, name="v_parts", tag="bank")
-        for c in range(CHUNKS):
-            r, k = divmod(c, P_CHUNKS)
-            nodes = slice(c * C_NODES, (c + 1) * C_NODES)
-            nc.tensor.matmul(v_parts[:, :, nodes], feat_flip[r][:, k, :], upper[:, :, nodes], start=True, stop=True)
+        for h in range(G_CHUNKS):
+            for g in range(GROUPS):
+                c = g * G_CHUNKS + h
+                r, k = divmod(c, P_CHUNKS)
+                nodes = slice(c * C_NODES, (c + 1) * C_NODES)
+                nc.tensor.matmul(
+                    v_parts[:, :, nodes], feat_flip[r][:, k, :], summands[h][:, :, g, :], start=True, stop=True
+                )
         v = held.tile([D, NODES], F32, name="v")
         nc.vector.tensor_reduce(v[:], v_parts[:].rearrange("d s p -> d p s"), axis=X, op=ALU.add)
 
-        neg = held.tile([D, NODES], F32, name="neg")
-        nc.vector.tensor_scalar_min(neg[:], v[:], 0.0)
-        exp_neg = held.tile([D, NODES], F32, name="exp_neg")
-        nc.scalar.activation(exp_neg[:], neg[:], ACT.Exp)
+        exp_v = held.tile([D, NODES], F32, name="exp_v")
+        nc.scalar.activation(exp_v[:], v[:], ACT.Exp)
         pos = held.tile([D, NODES], F32, name="pos")
         nc.vector.tensor_scalar(pos[:], v[:], 0.0, -1.0, op0=ALU.max, op1=ALU.add)
         res = held.tile([D, NODES], F32, name="res")
-        nc.vector.tensor_tensor(res[:], pos[:], exp_neg[:], op=ALU.add)
+        nc.vector.scalar_tensor_tensor(res[:], exp_v[:], 1.0, pos[:], op0=ALU.min, op1=ALU.add)
         nc.sync.dma_start(out, res[:])

@@ -64,7 +64,7 @@ def tile_sc_encoder_kernel(tc, table, h_ref, a_nei, a_ref, offs, out):
         nc.vector.tensor_scalar(others[:], own[:], -1.0, FAR, op0=ALU.add, op1=ALU.mult)
         w_nei = held.tile([D, GROUPS * (NODES + G_NODES)], BF16, name="w_nei")
         nc.vector.memset(w_nei[:], 0.0)
-        nc.vector.tensor_copy(
+        nc.gpsimd.tensor_copy(
             w_nei[:].rearrange("k (g r) -> k g r", g=GROUPS)[:, :, 0:G_NODES],
             anei_sb[:, 0:1].unsqueeze(2).to_broadcast([D, GROUPS, G_NODES]),
         )

@@ -132,22 +132,19 @@ def tile_sc_encoder_kernel(tc, table, h_ref, a_nei, a_ref, offs, out):
             nc.vector.tensor_copy(flipped[:], flip_ps[:])
             feat_flip.append(flipped)
 
-        v_parts = psum.tile([D, SUMMANDS, NODES], F32, name="v_parts", tag="bank")
+        res = held.tile([D, GROUPS, G_CHUNKS, C_NODES], F32, name="res")
         for h in range(G_CHUNKS):
+            v_parts = psum.tile([D, SUMMANDS, GROUPS, C_NODES], F32, name=f"v_parts{h}", tag="bank")
             for g in range(GROUPS):
-                c = g * G_CHUNKS + h
-                r, k = divmod(c, P_CHUNKS)
-                nodes = slice(c * C_NODES, (c + 1) * C_NODES)
+                r, k = divmod(g * G_CHUNKS + h, P_CHUNKS)
                 nc.tensor.matmul(
-                    v_parts[:, :, nodes], feat_flip[r][:, k, :], summands[h][:, :, g, :], start=True, stop=True
+                    v_parts[:, :, g, :], feat_flip[r][:, k, :], summands[h][:, :, g, :], start=True, stop=True
                 )
-        v = held.tile([D, NODES], F32, name="v")
-        nc.vector.tensor_reduce(v[:], v_parts[:].rearrange("d s p -> d p s"), axis=X, op=ALU.add)
-
-        exp_v = held.tile([D, NODES], F32, name="exp_v")
-        nc.scalar.activation(exp_v[:], v[:], ACT.Exp)
-        pos = held.tile([D, NODES], F32, name="pos")
-        nc.vector.tensor_scalar(pos[:], v[:], 0.0, -1.0, op0=ALU.max, op1=ALU.add)
-        res = held.tile([D, NODES], F32, name="res")
-        nc.vector.scalar_tensor_tensor(res[:], exp_v[:], 1.0, pos[:], op0=ALU.min, op1=ALU.add)
-        nc.sync.dma_start(out, res[:])
+            v = held.tile([D, GROUPS, C_NODES], F32, name=f"v{h}")
+            nc.vector.tensor_reduce(v[:], v_parts[:].rearrange("d s g n -> d g n s"), axis=X, op=ALU.add)
+            exp_v = held.tile([D, GROUPS, C_NODES], F32, name=f"exp_v{h}")
+            nc.scalar.activation(exp_v[:], v[:], ACT.Exp)
+            pos = held.tile([D, GROUPS, C_NODES], F32, name=f"pos{h}")
+            nc.vector.tensor_scalar(pos[:], v[:], 0.0, -1.0, op0=ALU.max, op1=ALU.add)
+            nc.vector.scalar_tensor_tensor(res[:, :, h, :], exp_v[:], 1.0, pos[:], op0=ALU.min, op1=ALU.add)
+        nc.sync.dma_start(out, res[:].rearrange("d g h n -> d (g h n)"))

@@ -31,6 +31,9 @@ C_NODES = CHUNK // NEI
 G_CHUNKS = CHUNKS // GROUPS
 P_CHUNKS = PIECE // CHUNK
 SUMMANDS = 3
+HALVES = 2
+H_NODES = NODES // HALVES
+H_CHUNKS = CHUNKS // HALVES
 
 PSUM_BANKS = 8
 
@@ -132,19 +135,21 @@ def tile_sc_encoder_kernel(tc, table, h_ref, a_nei, a_ref, offs, out):
             nc.vector.tensor_copy(flipped[:], flip_ps[:])
             feat_flip.append(flipped)
 
-        res = held.tile([D, GROUPS, G_CHUNKS, C_NODES], F32, name="res")
-        for h in range(G_CHUNKS):
-            v_parts = psum.tile([D, SUMMANDS, GROUPS, C_NODES], F32, name=f"v_parts{h}", tag="bank")
-            for g in range(GROUPS):
-                r, k = divmod(g * G_CHUNKS + h, P_CHUNKS)
+        res = held.tile([D, HALVES, H_NODES], F32, name="res")
+        for half in range(HALVES):
+            v_parts = psum.tile([D, SUMMANDS, H_CHUNKS, C_NODES], F32, name=f"v_parts{half}", tag="bank")
+            for i in range(H_CHUNKS):
+                c = half * H_CHUNKS + i
+                g, h = divmod(c, G_CHUNKS)
+                r, k = divmod(c, P_CHUNKS)
                 nc.tensor.matmul(
-                    v_parts[:, :, g, :], feat_flip[r][:, k, :], summands[h][:, :, g, :], start=True, stop=True
+                    v_parts[:, :, i, :], feat_flip[r][:, k, :], summands[h][:, :, g, :], start=True, stop=True
                 )
-            v = held.tile([D, GROUPS, C_NODES], F32, name=f"v{h}")
-            nc.vector.tensor_reduce(v[:], v_parts[:].rearrange("d s g n -> d g n s"), axis=X, op=ALU.add)
-            exp_v = held.tile([D, GROUPS, C_NODES], F32, name=f"exp_v{h}")
+            v = held.tile([D, H_NODES], F32, name=f"v{half}")
+            nc.vector.tensor_reduce(v[:], v_parts[:].rearrange("d s i n -> d (i n) s"), axis=X, op=ALU.add)
+            exp_v = held.tile([D, H_NODES], F32, name=f"exp_v{half}")
             nc.scalar.activation(exp_v[:], v[:], ACT.Exp)
-            pos = held.tile([D, GROUPS, C_NODES], F32, name=f"pos{h}")
+            pos = held.tile([D, H_NODES], F32, name=f"pos{half}")
             nc.vector.tensor_scalar(pos[:], v[:], 0.0, -1.0, op0=ALU.max, op1=ALU.add)
-            nc.vector.scalar_tensor_tensor(res[:, :, h, :], exp_v[:], 1.0, pos[:], op0=ALU.min, op1=ALU.add)
-        nc.sync.dma_start(out, res[:].rearrange("d g h n -> d (g h n)"))
+            nc.vector.scalar_tensor_tensor(res[:, half, :], exp_v[:], 1.0, pos[:], op0=ALU.min, op1=ALU.add)
+        nc.sync.dma_start(out, res[:].rearrange("d a n -> d (a n)"))

@@ -16,19 +16,22 @@ N = NODES * NEI
 SLOPE = 0.01
 FAR = 2.0**126
 
-GROUPS = 8
-G_NODES = NODES // GROUPS
+CHUNK = 128
+CHUNKS = N // CHUNK
+PLACES = CHUNK // NEI
+BLOCK = 32
+B_PLACES = BLOCK // CHUNKS
+BLOCKS = 128 // BLOCK
+
+GROUP_CHUNKS = 2
+GROUPS = CHUNKS // GROUP_CHUNKS
+G_NODES = GROUP_CHUNKS * PLACES
 G_ENTRIES = G_NODES * NEI
 G_COLS = G_ENTRIES // 16
 
 PIECE = 512
 PIECES = N // PIECE
 P_COLS = PIECE // 16
-
-CHUNK = 128
-CHUNKS = N // CHUNK
-C_NODES = CHUNK // NEI
-G_CHUNKS = CHUNKS // GROUPS
 P_CHUNKS = PIECE // CHUNK
 SUMMANDS = 3
 HALVES = 2
@@ -57,31 +60,54 @@ def tile_sc_encoder_kernel(tc, table, h_ref, a_nei, a_ref, offs, out):
         offsets = held.tile([128, N // 16], U16, name="offsets")
         nc.sync.dma_start(offsets[:], offs)
 
+        others = held.tile([NODES, G_NODES], BF16, name="others")
+        nc.gpsimd.memset(others[:], 0.0)
+        nc.gpsimd.affine_select(
+            others[:], others[:], compare_op=ALU.is_ge, fill=-FAR, base=0,
+            pattern=[[-GROUPS, G_NODES]], channel_multiplier=1,
+        )
+        nc.gpsimd.affine_select(
+            others[:], others[:], compare_op=ALU.is_ge, fill=-FAR, base=GROUPS - 1,
+            pattern=[[GROUPS, G_NODES]], channel_multiplier=-1,
+        )
         ident = held.tile([128, 128], BF16, name="ident")
         make_identity(nc, ident[:])
-        ident_f32 = held.tile([128, 128], F32, name="ident_f32")
-        make_identity(nc, ident_f32[:])
-        own = held.tile([NODES, G_NODES], F32, name="own")
-        nc.vector.tensor_reduce(own[:], ident[:].rearrange("p (g n) -> p n g", n=G_NODES), axis=X, op=ALU.add)
-        others = held.tile([NODES, G_NODES], BF16, name="others")
-        nc.vector.tensor_scalar(others[:], own[:], -1.0, FAR, op0=ALU.add, op1=ALU.mult)
-        w_nei = held.tile([D, GROUPS * (NODES + G_NODES)], BF16, name="w_nei")
+        w_nei = held.tile([D, G_NODES + 1, GROUPS], BF16, name="w_nei")
         nc.vector.memset(w_nei[:], 0.0)
-        nc.gpsimd.tensor_copy(
-            w_nei[:].rearrange("k (g r) -> k g r", g=GROUPS)[:, :, 0:G_NODES],
-            anei_sb[:, 0:1].unsqueeze(2).to_broadcast([D, GROUPS, G_NODES]),
+        nc.vector.tensor_copy(w_nei[:, :, 0], anei_sb[:, 0:1].to_broadcast([D, G_NODES + 1]))
+        w_nei_flat = w_nei[:].rearrange("k n g -> k (n g)")
+        place = held.tile([128, PLACES], F32, name="place")
+        nc.vector.tensor_reduce(place[:], ident[:].rearrange("p (c b) -> p c b", b=CHUNKS), axis=X, op=ALU.add)
+        mask = held.tile([128, PLACES, CHUNKS], F32, name="mask")
+        nc.vector.tensor_copy(mask[:], place[:].unsqueeze(2).to_broadcast([128, PLACES, CHUNKS]))
+        href_by_place = held.tile([D, PLACES, GROUP_CHUNKS, GROUPS], BF16, name="href_by_place")
+        nc.vector.tensor_copy(
+            href_by_place[:], href_sb[:].rearrange("k (g h c) -> k c h g", h=GROUP_CHUNKS, c=PLACES)
         )
 
         score = psum.tile([NODES, G_NODES, NEI], F32, name="score", tag="bank")
         score_flat = score[:].rearrange("p n t -> p (n t)")
         nc.tensor.matmul(
-            score[:], ident[:], others[:].unsqueeze(2).to_broadcast([NODES, G_NODES, NEI]), start=True, stop=False
+            score[:].rearrange("p (h c) t -> p h c t", c=PLACES),
+            ident[:],
+            others[:]
+            .rearrange("p (c h) -> p h c", c=PLACES)
+            .unsqueeze(3)
+            .to_broadcast([NODES, GROUP_CHUNKS, PLACES, NEI]),
+            start=True,
+            stop=False,
         )
-        nc.tensor.matmul(score_flat, href_sb[:], aref_sb[:, 0:1].to_broadcast([D, G_ENTRIES]), start=False, stop=False)
+        nc.tensor.matmul(
+            score_flat,
+            href_by_place[:].rearrange("k c h g -> k (c h g)"),
+            aref_sb[:, 0:1].to_broadcast([D, G_ENTRIES]),
+            start=False,
+            stop=False,
+        )
         for g in range(GROUPS):
             nc.tensor.matmul(
                 score_flat,
-                w_nei[:, g * NODES : (g + 1) * NODES],
+                w_nei_flat[:, GROUPS - g : GROUPS - g + NODES],
                 table_sb[:].indirect(offsets[:, g * G_COLS : (g + 1) * G_COLS]),
                 start=False,
                 stop=(g == GROUPS - 1),
@@ -96,57 +122,60 @@ def tile_sc_encoder_kernel(tc, table, h_ref, a_nei, a_ref, offs, out):
                 stop=True,
             )
 
-        minus_score = held.tile([NODES, G_ENTRIES], F32, name="minus_score")
-        minus_max = held.tile([NODES, 1], F32, name="minus_max")
-        nc.vector.tensor_scalar(
-            minus_score[:], score_flat, -1.0, None, op0=ALU.mult, op1=ALU.min, accum_out=minus_max[:]
-        )
-        minus_act = held.tile([NODES, G_ENTRIES], F32, name="minus_act")
-        nc.vector.scalar_tensor_tensor(minus_act[:], minus_score[:], SLOPE, minus_score[:], op0=ALU.mult, op1=ALU.min)
+        own_score = held.tile([NODES, NEI], F32, name="own_score")
+        nc.vector.tensor_reduce(own_score[:], score[:].rearrange("p n t -> p t n"), axis=X, op=ALU.max)
+        act = held.tile([NODES, NEI], F32, name="act", tag="act, then feat")
+        nc.vector.scalar_tensor_tensor(act[:], own_score[:], SLOPE, own_score[:], op0=ALU.mult, op1=ALU.max)
         minus_top = held.tile([NODES, 1], F32, name="minus_top")
-        nc.vector.scalar_tensor_tensor(minus_top[:], minus_max[:], SLOPE, minus_max[:], op0=ALU.mult, op1=ALU.min)
-        e = held.tile([NODES, G_ENTRIES], F32, name="e")
+        nc.vector.tensor_reduce(minus_top[:], act[:], axis=X, op=ALU.max, negate=True)
+        e = held.tile([NODES, NEI], F32, name="e")
         esum = held.tile([NODES, 1], F32, name="esum")
-        nc.scalar.activation(e[:], minus_act[:], ACT.Exp, bias=minus_top[:], scale=-1.0, accum_out=esum[:])
+        nc.scalar.activation(e[:], act[:], ACT.Exp, bias=minus_top[:], scale=1.0, accum_out=esum[:])
         rsum = held.tile([NODES, 1], F32, name="rsum")
         nc.vector.reciprocal(rsum[:], esum[:])
+        att = held.tile([NODES, B_PLACES, NEI], F32, name="att", align_bytes=64)
+        nc.vector.tensor_scalar_mul(
+            att[:], e[:].unsqueeze(1).to_broadcast([NODES, B_PLACES, NEI]), rsum[:, 0:1]
+        )
 
-        summands = []
-        for h in range(G_CHUNKS):
-            att = held.tile([NODES, CHUNK], F32, name=f"att{h}")
-            nc.vector.tensor_scalar_mul(att[:], e[:, h * CHUNK : (h + 1) * CHUNK], rsum[:, 0:1])
-            att_flip = psum.tile([CHUNK, GROUPS, G_CHUNKS, C_NODES], F32, name=f"att_flip{h}", tag="bank")
-            nc.tensor.transpose(att_flip[:].rearrange("j g i n -> j (g i n)"), att[:], ident_f32[:])
-            rest = held.tile([CHUNK, SUMMANDS, GROUPS, C_NODES], F32, name=f"rest{h}")
-            nc.vector.tensor_copy(rest[:, 0], att_flip[:, :, h, :])
-            upper = rest[:].bitcast(BF16).rearrange("j s g (n half) -> j s g n half", half=2)[:, :, :, :, 1]
-            for s in range(SUMMANDS - 1):
-                nc.vector.tensor_tensor(rest[:, s + 1], rest[:, s], upper[:, s], op=ALU.subtract)
-            summands.append(upper)
+        att_flip = held.tile([CHUNK, B_PLACES, CHUNKS], F32, name="att_flip", tag="att, then feat flip", align_bytes=64)
+        nc.vector.transpose(att_flip[:].rearrange("j i b -> j (i b)"), att[:].rearrange("p i t -> p (i t)"))
+        rest = held.tile([CHUNK, SUMMANDS, PLACES, CHUNKS], F32, name="rest")
+        nc.vector.tensor_tensor(
+            rest[:, 0].rearrange("j (a i) b -> j a (i b)", a=BLOCKS),
+            att_flip[:].rearrange("j i b -> j (i b)").unsqueeze(1).to_broadcast([CHUNK, BLOCKS, BLOCK]),
+            mask[:].rearrange("j (a i) b -> j a (i b)", a=BLOCKS),
+            op=ALU.mult,
+        )
+        upper = rest[:].bitcast(BF16).rearrange("j s c (b half) -> j s c b half", half=2)[:, :, :, :, 1]
+        for s in range(SUMMANDS - 1):
+            nc.vector.tensor_tensor(rest[:, s + 1], rest[:, s], upper[:, s], op=ALU.subtract)
 
-        feat_flip = []
+        feat_first = held.tile([D, P_CHUNKS, CHUNK], BF16, name="feat_first")
+        feat_others = held.tile([D, PIECES - 1, P_CHUNKS, CHUNK], BF16, name="feat_others", tag="act, then feat")
+        feat_sb = [feat_first[:]] + [feat_others[:, r] for r in range(PIECES - 1)]
+        feat_flip = held.tile(
+            [CHUNK, PIECES, P_CHUNKS, D], BF16, name="feat_flip", tag="att, then feat flip", align_bytes=64
+        )
         for r in range(PIECES):
-            feat_sb = held.tile([D, P_CHUNKS, CHUNK], BF16, name=f"feat_sb{r}")
-            nc.scalar.copy(feat_sb[:].rearrange("d k j -> d (k j)"), feats[r][:])
+            nc.scalar.copy(feat_sb[r].rearrange("d k j -> d (k j)"), feats[r][:])
             flip_ps = psum.tile([CHUNK, P_CHUNKS, D], BF16, name=f"flip_ps{r}", tag="bank")
             for k in range(P_CHUNKS):
-                nc.tensor.transpose(flip_ps[:, k, :], feat_sb[:, k, :], ident[:])
-            flipped = held.tile([CHUNK, P_CHUNKS, D], BF16, name=f"feat_flip{r}")
-            nc.vector.tensor_copy(flipped[:], flip_ps[:])
-            feat_flip.append(flipped)
+                nc.tensor.transpose(flip_ps[:, k, :], feat_sb[r][:, k, :], ident[:])
+            nc.vector.tensor_copy(feat_flip[:, r], flip_ps[:])
 
         res = held.tile([D, HALVES, H_NODES], F32, name="res")
         for half in range(HALVES):
-            v_parts = psum.tile([D, SUMMANDS, H_CHUNKS, C_NODES], F32, name=f"v_parts{half}", tag="bank")
+            v_parts = psum.tile([D, SUMMANDS, H_CHUNKS, PLACES], F32, name=f"v_parts{half}", tag="bank")
             for i in range(H_CHUNKS):
-                c = half * H_CHUNKS + i
-                g, h = divmod(c, G_CHUNKS)
-                r, k = divmod(c, P_CHUNKS)
+                b = half * H_CHUNKS + i
+                r, k = divmod(b, P_CHUNKS)
+                g, h = divmod(b, GROUP_CHUNKS)
                 nc.tensor.matmul(
-                    v_parts[:, :, i, :], feat_flip[r][:, k, :], summands[h][:, :, g, :], start=True, stop=True
+                    v_parts[:, :, i, :], feat_flip[:, r, k, :], upper[:, :, :, GROUPS * h + g], start=True, stop=True
                 )
             v = held.tile([D, H_NODES], F32, name=f"v{half}")
-            nc.vector.tensor_reduce(v[:], v_parts[:].rearrange("d s i n -> d (i n) s"), axis=X, op=ALU.add)
+            nc.vector.tensor_reduce(v[:], v_parts[:].rearrange("d s i c -> d (i c) s"), axis=X, op=ALU.add)
             exp_v = held.tile([D, H_NODES], F32, name=f"exp_v{half}")
             nc.scalar.activation(exp_v[:], v[:], ACT.Exp)
             pos = held.tile([D, H_NODES], F32, name=f"pos{half}")

@@ -19,9 +19,6 @@ FAR = 2.0**126
 CHUNK = 128
 CHUNKS = N // CHUNK
 PLACES = CHUNK // NEI
-BLOCK = 32
-B_PLACES = BLOCK // CHUNKS
-BLOCKS = 128 // BLOCK
 
 GROUP_CHUNKS = 2
 GROUPS = CHUNKS // GROUP_CHUNKS
@@ -29,10 +26,9 @@ G_NODES = GROUP_CHUNKS * PLACES
 G_ENTRIES = G_NODES * NEI
 G_COLS = G_ENTRIES // 16
 
-PIECE = 512
-PIECES = N // PIECE
-P_COLS = PIECE // 16
-P_CHUNKS = PIECE // CHUNK
+PIECE_CHUNKS = [4, 4, 4, 2, 2]
+CHUNK_COLS = CHUNK // 16
+SWAPPED = 1
 SUMMANDS = 3
 HALVES = 2
 H_NODES = NODES // HALVES
@@ -76,10 +72,10 @@ def tile_sc_encoder_kernel(tc, table, h_ref, a_nei, a_ref, offs, out):
         nc.vector.memset(w_nei[:], 0.0)
         nc.vector.tensor_copy(w_nei[:, :, 0], anei_sb[:, 0:1].to_broadcast([D, G_NODES + 1]))
         w_nei_flat = w_nei[:].rearrange("k n g -> k (n g)")
-        place = held.tile([128, PLACES], F32, name="place")
+        place = held.tile([NODES, PLACES], F32, name="place")
         nc.vector.tensor_reduce(place[:], ident[:].rearrange("p (c b) -> p c b", b=CHUNKS), axis=X, op=ALU.add)
-        mask = held.tile([128, PLACES, CHUNKS], F32, name="mask")
-        nc.vector.tensor_copy(mask[:], place[:].unsqueeze(2).to_broadcast([128, PLACES, CHUNKS]))
+        mask = held.tile([NODES, PLACES, NEI], F32, name="mask")
+        nc.vector.tensor_copy(mask[:], place[:].unsqueeze(2).to_broadcast([NODES, PLACES, NEI]))
         href_by_place = held.tile([D, PLACES, GROUP_CHUNKS, GROUPS], BF16, name="href_by_place")
         nc.vector.tensor_copy(
             href_by_place[:], href_sb[:].rearrange("k (g h c) -> k c h g", h=GROUP_CHUNKS, c=PLACES)
@@ -112,17 +108,18 @@ def tile_sc_encoder_kernel(tc, table, h_ref, a_nei, a_ref, offs, out):
                 start=False,
                 stop=(g == GROUPS - 1),
             )
-        feats = [psum.tile([D, PIECE], F32, name=f"feat{r}", tag="bank") for r in range(PIECES)]
-        for r in range(PIECES):
+        chunks = [slice(sum(PIECE_CHUNKS[:r]), sum(PIECE_CHUNKS[: r + 1])) for r in range(len(PIECE_CHUNKS))]
+        feats = [psum.tile([D, n, CHUNK], F32, name=f"feat{r}", tag="bank") for r, n in enumerate(PIECE_CHUNKS)]
+        for feat, piece in zip(feats, chunks):
             nc.tensor.matmul(
-                feats[r][:],
+                feat[:].rearrange("d k j -> d (k j)"),
                 ident[:],
-                table_sb[:].indirect(offsets[:, r * P_COLS : (r + 1) * P_COLS]),
+                table_sb[:].indirect(offsets[:, piece.start * CHUNK_COLS : piece.stop * CHUNK_COLS]),
                 start=True,
                 stop=True,
             )
 
-        own_score = held.tile([NODES, NEI], F32, name="own_score")
+        own_score = held.tile([NODES, NEI], F32, name="own_score", tag="own, then feat")
         nc.vector.tensor_reduce(own_score[:], score[:].rearrange("p n t -> p t n"), axis=X, op=ALU.max)
         act = held.tile([NODES, NEI], F32, name="act", tag="act, then feat")
         nc.vector.scalar_tensor_tensor(act[:], own_score[:], SLOPE, own_score[:], op0=ALU.mult, op1=ALU.max)
@@ -133,46 +130,41 @@ def tile_sc_encoder_kernel(tc, table, h_ref, a_nei, a_ref, offs, out):
         nc.scalar.activation(e[:], act[:], ACT.Exp, bias=minus_top[:], scale=1.0, accum_out=esum[:])
         rsum = held.tile([NODES, 1], F32, name="rsum")
         nc.vector.reciprocal(rsum[:], esum[:])
-        att = held.tile([NODES, B_PLACES, NEI], F32, name="att", align_bytes=64)
-        nc.vector.tensor_scalar_mul(
-            att[:], e[:].unsqueeze(1).to_broadcast([NODES, B_PLACES, NEI]), rsum[:, 0:1]
+        att = held.tile([NODES, PLACES, NEI], F32, name="att", tag="att, then feat flip", align_bytes=64)
+        nc.vector.scalar_tensor_tensor(
+            att[:], e[:].unsqueeze(1).to_broadcast([NODES, PLACES, NEI]), rsum[:, 0:1], mask[:], op0=ALU.mult, op1=ALU.mult
         )
 
-        att_flip = held.tile([CHUNK, B_PLACES, CHUNKS], F32, name="att_flip", tag="att, then feat flip", align_bytes=64)
-        nc.vector.transpose(att_flip[:].rearrange("j i b -> j (i b)"), att[:].rearrange("p i t -> p (i t)"))
-        rest = held.tile([CHUNK, SUMMANDS, PLACES, CHUNKS], F32, name="rest")
-        nc.vector.tensor_tensor(
-            rest[:, 0].rearrange("j (a i) b -> j a (i b)", a=BLOCKS),
-            att_flip[:].rearrange("j i b -> j (i b)").unsqueeze(1).to_broadcast([CHUNK, BLOCKS, BLOCK]),
-            mask[:].rearrange("j (a i) b -> j a (i b)", a=BLOCKS),
-            op=ALU.mult,
-        )
+        rest = held.tile([CHUNK, SUMMANDS, PLACES, CHUNKS], F32, name="rest", align_bytes=64)
+        nc.vector.transpose(rest[:, 0].rearrange("j c b -> j (c b)"), att[:].rearrange("p c t -> p (c t)"))
         upper = rest[:].bitcast(BF16).rearrange("j s c (b half) -> j s c b half", half=2)[:, :, :, :, 1]
         for s in range(SUMMANDS - 1):
             nc.vector.tensor_tensor(rest[:, s + 1], rest[:, s], upper[:, s], op=ALU.subtract)
 
-        feat_first = held.tile([D, P_CHUNKS, CHUNK], BF16, name="feat_first")
-        feat_others = held.tile([D, PIECES - 1, P_CHUNKS, CHUNK], BF16, name="feat_others", tag="act, then feat")
-        feat_sb = [feat_first[:]] + [feat_others[:, r] for r in range(PIECES - 1)]
-        feat_flip = held.tile(
-            [CHUNK, PIECES, P_CHUNKS, D], BF16, name="feat_flip", tag="att, then feat flip", align_bytes=64
-        )
-        for r in range(PIECES):
-            nc.scalar.copy(feat_sb[r].rearrange("d k j -> d (k j)"), feats[r][:])
-            flip_ps = psum.tile([CHUNK, P_CHUNKS, D], BF16, name=f"flip_ps{r}", tag="bank")
-            for k in range(P_CHUNKS):
+        feat_first = held.tile([D, PIECE_CHUNKS[0], CHUNK], BF16, name="feat_first")
+        feat_second = held.tile([D, PIECE_CHUNKS[1], CHUNK], BF16, name="feat_second", tag="own, then feat")
+        feat_later = held.tile([D, sum(PIECE_CHUNKS[2:]), CHUNK], BF16, name="feat_later", tag="act, then feat")
+        later = chunks[2].start
+        feat_sb = [feat_first[:], feat_second[:]]
+        feat_sb += [feat_later[:, piece.start - later : piece.stop - later] for piece in chunks[2:]]
+        feat_flip = held.tile([CHUNK, CHUNKS, D], BF16, name="feat_flip", tag="att, then feat flip", align_bytes=64)
+        for r, piece in enumerate(chunks):
+            copy = nc.vector.tensor_copy if r == SWAPPED else nc.scalar.copy
+            copy(feat_sb[r], feats[r][:])
+            flip_ps = psum.tile([CHUNK, PIECE_CHUNKS[r], D], BF16, name=f"flip_ps{r}", tag="bank")
+            for k in range(PIECE_CHUNKS[r]):
                 nc.tensor.transpose(flip_ps[:, k, :], feat_sb[r][:, k, :], ident[:])
-            nc.vector.tensor_copy(feat_flip[:, r], flip_ps[:])
+            copy = nc.scalar.copy if r == SWAPPED else nc.vector.tensor_copy
+            copy(feat_flip[:, piece], flip_ps[:])
 
         res = held.tile([D, HALVES, H_NODES], F32, name="res")
         for half in range(HALVES):
             v_parts = psum.tile([D, SUMMANDS, H_CHUNKS, PLACES], F32, name=f"v_parts{half}", tag="bank")
             for i in range(H_CHUNKS):
                 b = half * H_CHUNKS + i
-                r, k = divmod(b, P_CHUNKS)
                 g, h = divmod(b, GROUP_CHUNKS)
                 nc.tensor.matmul(
-                    v_parts[:, :, i, :], feat_flip[:, r, k, :], upper[:, :, :, GROUPS * h + g], start=True, stop=True
+                    v_parts[:, :, i, :], feat_flip[:, b, :], upper[:, :, :, GROUPS * h + g], start=True, stop=True
                 )
             v = held.tile([D, H_NODES], F32, name=f"v{half}")
             nc.vector.tensor_reduce(v[:], v_parts[:].rearrange("d s i c -> d (i c) s"), axis=X, op=ALU.add)

import concourse.mybir as mybir
from concourse.masks import make_identity

BF16 = mybir.dt.bfloat16
F32 = mybir.dt.float32
U16 = mybir.dt.uint16
ALU = mybir.AluOpType
ACT = mybir.ActivationFunctionType
X = mybir.AxisListType.X

D = 128
S = 1024
NODES = 128
NEI = 16
N = NODES * NEI
SLOPE = 0.01
FAR = 2.0**126

CHUNK = 128
CHUNKS = N // CHUNK
PLACES = CHUNK // NEI

GROUP_CHUNKS = 2
GROUPS = CHUNKS // GROUP_CHUNKS
G_NODES = GROUP_CHUNKS * PLACES
G_ENTRIES = G_NODES * NEI
G_COLS = G_ENTRIES // 16

PIECE_CHUNKS = [4, 4, 4, 2, 2]
CHUNK_COLS = CHUNK // 16
SWAPPED = 1
SUMMANDS = 3
HALVES = 2
H_NODES = NODES // HALVES
H_CHUNKS = CHUNKS // HALVES

PSUM_BANKS = 8

FLOPS = 2 * D * N + 2 * D * NODES + 2 * D * N


def tile_sc_encoder_kernel(tc, table, h_ref, a_nei, a_ref, offs, out):
    nc = tc.nc
    with (
        tc.tile_pool(name="held", bufs=1) as held,
        tc.psum_pool(name="psum", bufs=PSUM_BANKS) as psum,
    ):
        aref_sb = held.tile([D, 1], BF16, name="aref_sb")
        nc.sync.dma_start(aref_sb[:], a_ref)
        anei_sb = held.tile([D, 1], BF16, name="anei_sb")
        nc.scalar.dma_start(anei_sb[:], a_nei)
        table_sb = held.tile([D, S], BF16, name="table_sb")
        nc.scalar.dma_start(table_sb[:], table)
        href_sb = held.tile([D, NODES], BF16, name="href_sb")
        nc.sync.dma_start(href_sb[:], h_ref)
        offsets = held.tile([128, N // 16], U16, name="offsets")
        nc.sync.dma_start(offsets[:], offs)

        others = held.tile([NODES, G_NODES], BF16, name="others")
        nc.gpsimd.memset(others[:], 0.0)
        nc.gpsimd.affine_select(
            others[:], others[:], compare_op=ALU.is_ge, fill=-FAR, base=0,
            pattern=[[-GROUPS, G_NODES]], channel_multiplier=1,
        )
        nc.gpsimd.affine_select(
            others[:], others[:], compare_op=ALU.is_ge, fill=-FAR, base=GROUPS - 1,
            pattern=[[GROUPS, G_NODES]], channel_multiplier=-1,
        )
        ident = held.tile([128, 128], BF16, name="ident")
        make_identity(nc, ident[:])
        w_nei = held.tile([D, G_NODES + 1, GROUPS], BF16, name="w_nei")
        nc.vector.memset(w_nei[:], 0.0)
        nc.vector.tensor_copy(w_nei[:, :, 0], anei_sb[:, 0:1].to_broadcast([D, G_NODES + 1]))
        w_nei_flat = w_nei[:].rearrange("k n g -> k (n g)")
        place = held.tile([NODES, PLACES], F32, name="place")
        nc.vector.tensor_reduce(place[:], ident[:].rearrange("p (c b) -> p c b", b=CHUNKS), axis=X, op=ALU.add)
        mask = held.tile([NODES, PLACES, NEI], F32, name="mask")
        nc.vector.tensor_copy(mask[:], place[:].unsqueeze(2).to_broadcast([NODES, PLACES, NEI]))
        href_by_place = held.tile([D, PLACES, GROUP_CHUNKS, GROUPS], BF16, name="href_by_place")
        nc.vector.tensor_copy(
            href_by_place[:], href_sb[:].rearrange("k (g h c) -> k c h g", h=GROUP_CHUNKS, c=PLACES)
        )

        score = psum.tile([NODES, G_NODES, NEI], F32, name="score", tag="bank")
        score_flat = score[:].rearrange("p n t -> p (n t)")
        nc.tensor.matmul(
            score[:].rearrange("p (h c) t -> p h c t", c=PLACES),
            ident[:],
            others[:]
            .rearrange("p (c h) -> p h c", c=PLACES)
            .unsqueeze(3)
            .to_broadcast([NODES, GROUP_CHUNKS, PLACES, NEI]),
            start=True,
            stop=False,
        )
        nc.tensor.matmul(
            score_flat,
            href_by_place[:].rearrange("k c h g -> k (c h g)"),
            aref_sb[:, 0:1].to_broadcast([D, G_ENTRIES]),
            start=False,
            stop=False,
        )
        for g in range(GROUPS):
            nc.tensor.matmul(
                score_flat,
                w_nei_flat[:, GROUPS - g : GROUPS - g + NODES],
                table_sb[:].indirect(offsets[:, g * G_COLS : (g + 1) * G_COLS]),
                start=False,
                stop=(g == GROUPS - 1),
            )
        chunks = [slice(sum(PIECE_CHUNKS[:r]), sum(PIECE_CHUNKS[: r + 1])) for r in range(len(PIECE_CHUNKS))]
        feats = [psum.tile([D, n, CHUNK], F32, name=f"feat{r}", tag="bank") for r, n in enumerate(PIECE_CHUNKS)]
        for feat, piece in zip(feats, chunks):
            nc.tensor.matmul(
                feat[:].rearrange("d k j -> d (k j)"),
                ident[:],
                table_sb[:].indirect(offsets[:, piece.start * CHUNK_COLS : piece.stop * CHUNK_COLS]),
                start=True,
                stop=True,
            )

        own_score = held.tile([NODES, NEI], F32, name="own_score", tag="own, then feat")
        nc.vector.tensor_reduce(own_score[:], score[:].rearrange("p n t -> p t n"), axis=X, op=ALU.max)
        act = held.tile([NODES, NEI], F32, name="act", tag="act, then feat")
        nc.vector.scalar_tensor_tensor(act[:], own_score[:], SLOPE, own_score[:], op0=ALU.mult, op1=ALU.max)
        minus_top = held.tile([NODES, 1], F32, name="minus_top")
        nc.vector.tensor_reduce(minus_top[:], act[:], axis=X, op=ALU.max, negate=True)
        e = held.tile([NODES, NEI], F32, name="e")
        esum = held.tile([NODES, 1], F32, name="esum")
        nc.scalar.activation(e[:], act[:], ACT.Exp, bias=minus_top[:], scale=1.0, accum_out=esum[:])
        rsum = held.tile([NODES, 1], F32, name="rsum")
        nc.vector.reciprocal(rsum[:], esum[:])
        att = held.tile([NODES, PLACES, NEI], F32, name="att", tag="att, then feat flip", align_bytes=64)
        nc.vector.scalar_tensor_tensor(
            att[:], e[:].unsqueeze(1).to_broadcast([NODES, PLACES, NEI]), rsum[:, 0:1], mask[:], op0=ALU.mult, op1=ALU.mult
        )

        rest = held.tile([CHUNK, SUMMANDS, PLACES, CHUNKS], F32, name="rest", align_bytes=64)
        nc.vector.transpose(rest[:, 0].rearrange("j c b -> j (c b)"), att[:].rearrange("p c t -> p (c t)"))
        upper = rest[:].bitcast(BF16).rearrange("j s c (b half) -> j s c b half", half=2)[:, :, :, :, 1]
        for s in range(SUMMANDS - 1):
            nc.vector.tensor_tensor(rest[:, s + 1], rest[:, s], upper[:, s], op=ALU.subtract)

        feat_first = held.tile([D, PIECE_CHUNKS[0], CHUNK], BF16, name="feat_first")
        feat_second = held.tile([D, PIECE_CHUNKS[1], CHUNK], BF16, name="feat_second", tag="own, then feat")
        feat_later = held.tile([D, sum(PIECE_CHUNKS[2:]), CHUNK], BF16, name="feat_later", tag="act, then feat")
        later = chunks[2].start
        feat_sb = [feat_first[:], feat_second[:]]
        feat_sb += [feat_later[:, piece.start - later : piece.stop - later] for piece in chunks[2:]]
        feat_flip = held.tile([CHUNK, CHUNKS, D], BF16, name="feat_flip", tag="att, then feat flip", align_bytes=64)
        for r, piece in enumerate(chunks):
            copy = nc.vector.tensor_copy if r == SWAPPED else nc.scalar.copy
            copy(feat_sb[r], feats[r][:])
            flip_ps = psum.tile([CHUNK, PIECE_CHUNKS[r], D], BF16, name=f"flip_ps{r}", tag="bank")
            for k in range(PIECE_CHUNKS[r]):
                nc.tensor.transpose(flip_ps[:, k, :], feat_sb[r][:, k, :], ident[:])
            copy = nc.scalar.copy if r == SWAPPED else nc.vector.tensor_copy
            copy(feat_flip[:, piece], flip_ps[:])

        res = held.tile([D, HALVES, H_NODES], F32, name="res")
        for half in range(HALVES):
            v_parts = psum.tile([D, SUMMANDS, H_CHUNKS, PLACES], F32, name=f"v_parts{half}", tag="bank")
            for i in range(H_CHUNKS):
                b = half * H_CHUNKS + i
                g, h = divmod(b, GROUP_CHUNKS)
                nc.tensor.matmul(
                    v_parts[:, :, i, :], feat_flip[:, b, :], upper[:, :, :, GROUPS * h + g], start=True, stop=True
                )
            v = held.tile([D, H_NODES], F32, name=f"v{half}")
            nc.vector.tensor_reduce(v[:], v_parts[:].rearrange("d s i c -> d (i c) s"), axis=X, op=ALU.add)
            exp_v = held.tile([D, H_NODES], F32, name=f"exp_v{half}")
            nc.scalar.activation(exp_v[:], v[:], ACT.Exp)
            pos = held.tile([D, H_NODES], F32, name=f"pos{half}")
            nc.vector.tensor_scalar(pos[:], v[:], 0.0, -1.0, op0=ALU.max, op1=ALU.add)
            nc.vector.scalar_tensor_tensor(res[:, half, :], exp_v[:], 1.0, pos[:], op0=ALU.min, op1=ALU.add)
        nc.sync.dma_start(out, res[:].rearrange("d a n -> d (a n)"))
